import numpy as np
import ml_dtypes


def mxq(x, axis, fmt="e4m3"):
    dtype, down = {"e4m3": (ml_dtypes.float8_e4m3fn, 7), "e5m2": (ml_dtypes.float8_e5m2, 14)}[fmt]
    v = np.moveaxis(np.asarray(x, np.float32).astype(ml_dtypes.bfloat16).astype(np.float64), axis, -1)
    blocks = v.reshape(v.shape[:-1] + (-1, 32))
    amax = np.abs(blocks).max(-1, keepdims=True)
    byte = np.maximum(np.where(amax > 0, np.frexp(amax)[1] - 1 + 127, 0) - down, 1)
    scale = np.exp2(byte - 127.0)
    codes = (blocks / scale).astype(np.float32).astype(dtype).astype(np.float64)
    return np.moveaxis((codes * scale).reshape(v.shape), -1, axis)


WIDE = False


def mx_kscale(k):
    if not WIDE:
        return np.ones(k)
    levels = np.array([10, -10, 5, -5, 0])
    if k % 512:
        return np.exp2(np.random.permutation(np.resize(levels, k // 32))).repeat(32)
    a = np.empty((k // 512, 16))
    for p in range(k // 512):
        a[p, :8] = np.random.permutation(np.resize(levels, 8))
        for g in range(8):
            far = levels[np.abs(levels - a[p, g]) >= 10]
            a[p, g + 8] = far[np.random.randint(len(far))]
    return np.exp2(a.ravel()).repeat(32)


BF16 = ml_dtypes.bfloat16


def bf(x):
    return np.asarray(x, np.float32).astype(BF16)


def f64(x):
    return np.asarray(x).astype(np.float64)


B, N, HD, ED, F = 1, 64, 128, 256, 1024
TD = HD + HD
MD = TD + ED
EPS = 1e-5


def layer_norm(x, g, b):
    mu = x.mean(-1, keepdims=True)
    var = x.var(-1, keepdims=True)
    return (x - mu) * (1.0 / np.sqrt(var + EPS)) * g + b


def setup_inputs():
    s = mx_kscale(MD)
    sx, se = s[:HD], s[TD:]
    sr = np.concatenate([sx, sx, se])
    return {"p": bf(np.random.standard_normal((B, N, N, ED)) + 0.5 * np.random.standard_normal((B, N, N))[..., None]),
            "x_down": bf(np.random.standard_normal((B, N, HD)) * sx),
            "ln_edge_g": bf((1.0 + 0.1 * np.random.standard_normal(ED)) * se),
            "ln_edge_b": bf(0.1 * np.random.standard_normal(ED) * se),
            "W1": bf(np.random.standard_normal((MD, F)) / np.sqrt(MD) / sr[:, None]),
            "b1": bf(0.1 * np.random.standard_normal(F))}


def reference(p, x_down, ln_edge_g, ln_edge_b, W1, b1):
    p_ln = layer_norm(f64(p), f64(ln_edge_g), f64(ln_edge_b))
    xd = f64(x_down)
    edge_bias = np.concatenate([np.broadcast_to(xd[:, :, None, :], (B, N, N, HD)),
                                np.broadcast_to(xd[:, None, :, :], (B, N, N, HD))], axis=-1)
    z_in = np.concatenate([edge_bias, p_ln], axis=-1)
    return np.maximum((mxq(z_in, 3, "e4m3") @ mxq(f64(W1), 0, "e4m3")) + f64(b1), 0.0)

@@ -1,0 +1,316 @@
+import concourse.mybir as mybir
+from concourse.masks import make_identity
+
+F32 = mybir.dt.float32
+BF16 = mybir.dt.bfloat16
+I32 = mybir.dt.int32
+U32 = mybir.dt.uint32
+U8 = mybir.dt.uint8
+FP8X4 = mybir.dt.float8_e4m3fn_x4
+ALU = mybir.AluOpType
+ACT = mybir.ActivationFunctionType
+
+P = 128
+PACK = 4
+NODES = 64
+HD = 128
+ED = 256
+F = 1024
+EDGES = NODES * NODES
+TILES = EDGES // P
+GROUPS = 4
+PER_GROUP = TILES // GROUPS
+N_BANK = 512
+EPS = 1e-5
+QUAD = 4
+QUADS = TILES // QUAD
+XP = HD // PACK
+EP = ED // PACK
+
+FLOPS = 2 * EDGES * (2 * HD + ED) * F
+
+
+def tile_edgeupdaterwrapper_v01_pa_t_kernel(tc, p, x_down, ln_edge_g, ln_edge_b, W1, b1, out):
+    nc = tc.nc
+    p_view = p.rearrange("b i j f -> (b i j) f").rearrange("(g m s) f -> g m s f", g=GROUPS, s=PER_GROUP)
+    out_view = out.rearrange("b i j f -> (b i j) f").rearrange("(g m s) f -> g m s f", g=GROUPS, s=PER_GROUP)
+
+    with tc.manual_schedule(), tc.tile_pool(name="keep", bufs=1) as keep:
+        rows = keep.tile([P, 4 * HD], BF16)
+        nc.vector.memset(rows[NODES:P, :], 0.0)
+        nc.sync.dma_start(
+            out=rows[0:NODES, :].rearrange("n (r f) -> n r f", r=4),
+            in_=x_down.rearrange("b n f -> (b n) f").unsqueeze(1).to_broadcast([NODES, 4, HD]),
+        )
+        for r, vec in ((0, ln_edge_g), (1, ln_edge_b)):
+            for h in range(2):
+                nc.sync.dma_start(
+                    out=rows[NODES + r : NODES + r + 1, h * ED : (h + 1) * ED],
+                    in_=vec.rearrange("(o f) -> o f", o=1),
+                )
+        p_sb = keep.tile([P, TILES, ED], BF16)
+        w_view = W1.rearrange("(q c) n -> q c n", c=PACK)
+        w_raw = keep.tile([P, PACK, F], BF16)
+        b1_bc = keep.tile([P, F], BF16)
+
+        def load_p(t0, n):
+            g, s = t0 // PER_GROUP, t0 % PER_GROUP
+            nc.sync.dma_start(out=p_sb[:, t0 : t0 + n, :], in_=p_view[g][:, s : s + n, :])
+
+        load_p(0, QUAD)
+        nc.sync.dma_start(out=w_raw[:, :, 0:N_BANK], in_=w_view[:, :, 0:N_BANK])
+        nc.sync.dma_start(out=w_raw[:, :, N_BANK:F], in_=w_view[:, :, N_BANK:F])
+        load_p(QUAD, QUAD)
+        load_p(8, 8)
+        nc.sync.dma_start(out=b1_bc[:], in_=b1.partition_broadcast(P))
+        load_p(16, 8)
+        load_p(24, 8)
+
+        ident = keep.tile([P, P], F32)
+        make_identity(nc, ident[:])
+        eps = keep.tile([P, 1], F32)
+        nc.vector.memset(eps[:], EPS)
+
+        used = NODES + 2
+        xg = keep.tile([P, used, PACK], BF16)
+        gain_bias = keep.tile([P, 2, PACK], F32)
+        with tc.psum_pool(name="psum_setup", bufs=1) as psum_setup:
+            words_t = psum_setup.tile([P, 2, P], F32)
+            words = rows[:].bitcast(F32)
+            for u in range(2):
+                nc.tensor.transpose(out=words_t[:, u, :], in_=words[:, u : 2 * P : 2], identity=ident[:])
+            nc.vector.tensor_copy(
+                out=xg[:].rearrange("q r c -> q (r c)").bitcast(F32).rearrange("q (r u) -> q r u", u=2),
+                in_=words_t[:, :, 0:used].rearrange("q u r -> q r u"),
+            )
+        nc.vector.tensor_copy(out=gain_bias[:], in_=xg[:, NODES:used, :])
+
+        tb = keep.tile([P, GROUPS, P, PACK], BF16, align_bytes=64)
+        tb_codes = keep.tile([P, GROUPS, P], U32, align_bytes=64)
+        tb_scales = keep.tile([P, GROUPS, P], U8, align_bytes=64)
+        nc.gpsimd.memset(tb_scales[:].rearrange("q s m -> q (s m)").bitcast(I32), 0)
+        nc.gpsimd.tensor_scalar(
+            out=tb[:].rearrange("q s (a b) c -> q (s a) b c", b=8),
+            in0=xg[:, 0:NODES, :].unsqueeze(2).to_broadcast([P, NODES, 8, PACK]),
+            scalar1=1.0, scalar2=0.0, op0=ALU.mult, op1=ALU.add,
+        )
+
+        def node_j(odd, engine_copy):
+            part = slice(XP * (1 + odd), XP * (2 + odd))
+            for h in range(2):
+                for pr in range(2):
+                    s = QUAD * odd + 2 * pr + h
+                    engine_copy(
+                        out=tb[part, 2 * h + pr, :, :].rearrange("q (a b) c -> q a b c", b=8),
+                        in_=xg[part, s:NODES:8, :].unsqueeze(1).to_broadcast([XP, 16, 8, PACK]),
+                    )
+
+        z_codes = keep.tile([P, QUADS, 2, 2, P], U32, align_bytes=64)
+        z_scales = keep.tile([P, QUADS, 2, 2, P], U8, align_bytes=64)
+
+        def node_operands():
+            nc.vector.quantize_mx(
+                out=tb_codes[:].rearrange("q s m -> q (s m)").bitcast(FP8X4),
+                scales=tb_scales[:].rearrange("q s m -> q (s m)"),
+                in_=tb[:].rearrange("q s m c -> q (s m c)"),
+            )
+
+        def place_i(g):
+            for src, dst in ((tb_codes, z_codes), (tb_scales, z_scales)):
+                nc.sync.dma_start(
+                    out=dst[0:XP, 2 * g : 2 * g + 2].rearrange("q k h r m -> q (k h r) m").bitcast(I32),
+                    in_=src[0:XP, g, :].bitcast(I32).unsqueeze(1).to_broadcast([XP, PER_GROUP, P if src is tb_codes else P // 4]),
+                )
+
+        def place_j(odd):
+            part = slice(XP * (1 + odd), XP * (2 + odd))
+            for src, dst in ((tb_codes, z_codes), (tb_scales, z_scales)):
+                nc.sync.dma_start(
+                    out=dst[XP : 2 * XP, odd:QUADS:2].rearrange("q k h r m -> q k (h r m)").bitcast(I32),
+                    in_=src[part].rearrange("q s m -> q (s m)").bitcast(I32).unsqueeze(1).to_broadcast(
+                        [XP, GROUPS, QUAD * P if src is tb_codes else QUAD * P // 4]),
+                )
+
+        w_grouped = keep.tile([P, F, PACK], BF16, align_bytes=64)
+        w_codes = keep.tile([P, F], U32, align_bytes=64)
+        w_scales = keep.tile([P, F], U8, align_bytes=64)
+
+        def bank(nh):
+            return slice(nh * N_BANK, (nh + 1) * N_BANK)
+
+        def quantise_weights(nh):
+            nc.vector.quantize_mx(
+                out=w_codes[:, bank(nh)].bitcast(FP8X4), scales=w_scales[:, bank(nh)],
+                in_=w_grouped[:, bank(nh), :].rearrange("q n c -> q (n c)"),
+            )
+
+        stats = keep.tile([P, TILES, 6], F32)
+        mean_var = keep.tile([P, TILES, 2], F32)
+        rstd = keep.tile([P, TILES], F32)
+        shift = keep.tile([P, TILES], F32)
+        u_codes = [keep.tile([P, 2 * P], U32, align_bytes=64, name="u_codes%d" % n) for n in range(2)]
+        u_scales = [keep.tile([P, 2 * P], U8, align_bytes=64, name="u_scales%d" % n) for n in range(2)]
+        for n in range(2):
+            nc.vector.memset(u_scales[n][:].bitcast(I32), 0)
+
+        with tc.tile_pool(name="work", bufs=2) as work, tc.tile_pool(name="outs", bufs=8) as outs, \
+                tc.psum_pool(name="psum_t", bufs=1) as psum_t, tc.psum_pool(name="psum_mm", bufs=6) as psum_mm:
+            normed_of = {}
+            turned_of = {}
+            planes_of = {}
+            grouped_of = {}
+            acc_of = {}
+            result_of = {}
+
+            def quad(k):
+                return slice(k * QUAD, (k + 1) * QUAD)
+
+            def sums(t):
+                nc.vector.bn_stats(out=stats[:, t, :], in_=p_sb[:, t, :])
+
+            def mean_and_variance(k):
+                for t in range(k * QUAD, (k + 1) * QUAD):
+                    nc.vector.bn_aggr(out=mean_var[:, t, :], in_=stats[:, t, :])
+
+            def scale(k):
+                nc.scalar.activation(
+                    out=rstd[:, quad(k)], in_=mean_var[:, quad(k), 1], func=ACT.Abs_reciprocal_sqrt, bias=eps[:, 0:1], scale=1.0
+                )
+
+            def shift_by_mean(k):
+                nc.vector.scalar_tensor_tensor(
+                    out=shift[:, quad(k)], in0=mean_var[:, quad(k), 0], scalar=-1.0, in1=rstd[:, quad(k)], op0=ALU.mult, op1=ALU.mult
+                )
+
+            def normalise(k, a):
+                if a == 0:
+                    normed_of[k] = work.tile([P, 2, PACK, 2, EP], F32, name="normed")
+                t = k * QUAD + a
+                nc.scalar.activation(
+                    out=normed_of[k][:, a // 2, :, a % 2, :], in_=p_sb[:, t, :].rearrange("m (q c) -> m c q", c=PACK),
+                    func=ACT.Identity, bias=shift[:, t : t + 1], scale=rstd[:, t : t + 1],
+                )
+
+            def transpose(k):
+                normed = normed_of.pop(k)
+                turned = [psum_t.tile([P, 2, 2, P], F32, name="turned%d" % n) for n in range(2)]
+                for c in range(PACK):
+                    for pr in range(2):
+                        nc.tensor.transpose(
+                            out=turned[c // 2][:, c % 2, pr, :], in_=normed[:, pr, c, :, :].rearrange("m h q -> m (h q)"),
+                            identity=ident[:],
+                        )
+                turned_of[k] = turned
+
+            def affine(k, c):
+                if c == 0:
+                    planes_of[k] = work.tile([P, PACK, 2 * P], BF16, name="planes")
+                nc.scalar.activation(
+                    out=planes_of[k][:, c, :], in_=turned_of[k][c // 2][:, c % 2, :, :].rearrange("q r m -> q (r m)"),
+                    func=ACT.Identity, bias=gain_bias[:, 1, c : c + 1], scale=gain_bias[:, 0, c : c + 1],
+                )
+
+            def group(k):
+                grouped = work.tile([P, 2 * P, PACK], BF16, align_bytes=64, name="grouped")
+                nc.gpsimd.tensor_scalar(
+                    out=grouped[:], in0=planes_of.pop(k)[:].rearrange("q c e -> q e c"),
+                    scalar1=1.0, scalar2=0.0, op0=ALU.mult, op1=ALU.add,
+                )
+                grouped_of[k] = grouped
+
+            def quantise(k):
+                nc.vector.quantize_mx(
+                    out=u_codes[k % 2][:].bitcast(FP8X4), scales=u_scales[k % 2][:],
+                    in_=grouped_of.pop(k)[:].rearrange("q e c -> q (e c)"),
+                )
+
+            def place(k):
+                for h in range(2):
+                    half = slice(h * EP, (h + 1) * EP)
+                    for src, dst in ((u_codes[k % 2], z_codes), (u_scales[k % 2], z_scales)):
+                        nc.sync.dma_start(
+                            out=dst[EP:P, k, h].rearrange("q r m -> q (r m)").bitcast(I32), in_=src[half, :].bitcast(I32)
+                        )
+
+            def place_of(t):
+                return t // QUAD, t % 2, (t % QUAD) // 2
+
+            def multiply(t):
+                k, h, pr = place_of(t)
+                for nh in range(2):
+                    acc = psum_mm.tile([P, N_BANK], F32)
+                    nc.tensor.matmul_mx(
+                        out=acc[:],
+                        lhsT=z_codes[:, k, h, pr, :].bitcast(FP8X4), lhsT_scale=z_scales[:, k, h, pr, :],
+                        rhs=w_codes[:, bank(nh)].bitcast(FP8X4), rhs_scale=w_scales[:, bank(nh)],
+                        start=True, stop=True,
+                    )
+                    acc_of[(t, nh)] = acc
+
+            def add_bias(t, nh):
+                if nh == 0:
+                    result_of[t] = outs.tile([P, F], F32, name="result")
+                nc.vector.tensor_tensor(
+                    out=result_of[t][:, bank(nh)], in0=acc_of.pop((t, nh))[:], in1=b1_bc[:, bank(nh)], op=ALU.add
+                )
+
+            def relu_and_store(t):
+                result = result_of.pop(t)
+                nc.scalar.activation(out=result[:, bank(0)], in_=result[:, bank(0)], func=ACT.Relu)
+                nc.gpsimd.tensor_scalar(
+                    out=result[:, bank(1)], in0=result[:, bank(1)],
+                    scalar1=float("inf"), scalar2=0.0, op0=ALU.min, op1=ALU.max,
+                )
+                nc.sync.dma_start(out=out_view[t // PER_GROUP][:, t % PER_GROUP, :], in_=result[:])
+
+            def is_quad(k):
+                return 0 <= k < QUADS
+
+            def is_tile(t):
+                return 0 <= t < TILES
+
+            for r in range(-3, QUADS + 1):
+                if r == -2:
+                    node_j(0, nc.vector.tensor_copy)
+                    nc.vector.tensor_copy(out=w_grouped[:, bank(0), :], in_=w_raw[:, :, bank(0)].rearrange("q c n -> q n c"))
+                    nc.scalar.copy(out=w_grouped[:, bank(1), :], in_=w_raw[:, :, bank(1)].rearrange("q c n -> q n c"))
+                if r == -1:
+                    node_j(1, nc.vector.tensor_copy)
+                    node_operands()
+                    place_i(0)
+                    place_j(0)
+                    place_j(1)
+                    for g in range(1, GROUPS):
+                        place_i(g)
+                    quantise_weights(0)
+                    quantise_weights(1)
+                for j in range(QUAD):
+                    t = QUAD * r + j
+                    if j == 0 and is_quad(r + 1):
+                        group(r + 1)
+                    if is_tile(t):
+                        multiply(t)
+                        add_bias(t, 0)
+                    if j == 1 and is_quad(r + 1):
+                        quantise(r + 1)
+                        place(r + 1)
+                    if j < 2 and is_quad(r + 3):
+                        sums(QUAD * (r + 3) + 2 * j)
+                        sums(QUAD * (r + 3) + 2 * j + 1)
+                    if is_tile(t):
+                        add_bias(t, 1)
+                    if j == 2 and is_quad(r + 3):
+                        mean_and_variance(r + 3)
+                    if j == 3 and is_quad(r + 3):
+                        scale(r + 3)
+                        shift_by_mean(r + 3)
+                    if is_tile(t - 1):
+                        relu_and_store(t - 1)
+                    if j < 2 and is_quad(r + 2):
+                        normalise(r + 2, 2 * j)
+                        normalise(r + 2, 2 * j + 1)
+                    if j == 1 and is_quad(r + 2):
+                        transpose(r + 2)
+                    if j >= 2 and is_quad(r + 2):
+                        affine(r + 2, 2 * (j - 2))
+                        affine(r + 2, 2 * (j - 2) + 1)

@@ -24,6 +24,9 @@ N_BANK = 512
 EPS = 1e-5
 QUAD = 4
 QUADS = TILES // QUAD
+RING = 4
+SCALAR_STATS = 1
+SCALAR_COLS = 384
 XP = HD // PACK
 EP = ED // PACK
 
@@ -36,33 +39,32 @@ def tile_edgeupdaterwrapper_v01_pa_t_kernel(tc, p, x_down, ln_edge_g, ln_edge_b,
     out_view = out.rearrange("b i j f -> (b i j) f").rearrange("(g m s) f -> g m s f", g=GROUPS, s=PER_GROUP)
 
     with tc.manual_schedule(), tc.tile_pool(name="keep", bufs=1) as keep:
+        p_sb = keep.tile([P, TILES, ED], BF16)
+        w_view = W1.rearrange("(q c) n -> q c n", c=PACK)
+        w_raw = keep.tile([P, PACK, F], BF16)
         rows = keep.tile([P, 4 * HD], BF16)
+        gain_raw = keep.tile([P, 2, 16], BF16)
+        b1_row = keep.tile([P, F], BF16)
+
+        def load_p(t0, n):
+            g, s = t0 // PER_GROUP, t0 % PER_GROUP
+            nc.sync.dma_start(out=p_sb[:, t0 : t0 + n, :], in_=p_view[g][:, s : s + n, :])
+
         nc.vector.memset(rows[NODES:P, :], 0.0)
+        nc.gpsimd.memset(b1_row[:].bitcast(I32), 0)
+        load_p(0, QUAD)
         nc.sync.dma_start(
             out=rows[0:NODES, :].rearrange("n (r f) -> n r f", r=4),
             in_=x_down.rearrange("b n f -> (b n) f").unsqueeze(1).to_broadcast([NODES, 4, HD]),
         )
         for r, vec in ((0, ln_edge_g), (1, ln_edge_b)):
             for h in range(2):
-                nc.sync.dma_start(
-                    out=rows[NODES + r : NODES + r + 1, h * ED : (h + 1) * ED],
-                    in_=vec.rearrange("(o f) -> o f", o=1),
-                )
-        p_sb = keep.tile([P, TILES, ED], BF16)
-        w_view = W1.rearrange("(q c) n -> q c n", c=PACK)
-        w_raw = keep.tile([P, PACK, F], BF16)
-        b1_bc = keep.tile([P, F], BF16)
-
-        def load_p(t0, n):
-            g, s = t0 // PER_GROUP, t0 % PER_GROUP
-            nc.sync.dma_start(out=p_sb[:, t0 : t0 + n, :], in_=p_view[g][:, s : s + n, :])
-
-        load_p(0, QUAD)
+                nc.sync.dma_start(out=gain_raw[h * EP : (h + 1) * EP, r, 0:PACK], in_=vec.rearrange("(q c) -> q c", c=PACK))
         nc.sync.dma_start(out=w_raw[:, :, 0:N_BANK], in_=w_view[:, :, 0:N_BANK])
         nc.sync.dma_start(out=w_raw[:, :, N_BANK:F], in_=w_view[:, :, N_BANK:F])
+        nc.sync.dma_start(out=b1_row[0:1, :], in_=b1.rearrange("(o f) -> o f", o=1))
         load_p(QUAD, QUAD)
         load_p(8, 8)
-        nc.sync.dma_start(out=b1_bc[:], in_=b1.partition_broadcast(P))
         load_p(16, 8)
         load_p(24, 8)
 
@@ -70,30 +72,35 @@ def tile_edgeupdaterwrapper_v01_pa_t_kernel(tc, p, x_down, ln_edge_g, ln_edge_b,
         make_identity(nc, ident[:])
         eps = keep.tile([P, 1], F32)
         nc.vector.memset(eps[:], EPS)
+        ones = keep.tile([P, P], BF16)
+        nc.vector.memset(ones[:], 1.0)
+        b1_bc = keep.tile([P, F], BF16)
 
-        used = NODES + 2
-        xg = keep.tile([P, used, PACK], BF16)
+        xg = keep.tile([P, NODES, PACK], BF16)
         gain_bias = keep.tile([P, 2, PACK], F32)
-        with tc.psum_pool(name="psum_setup", bufs=1) as psum_setup:
-            words_t = psum_setup.tile([P, 2, P], F32)
+
+        def turn_rows(words_t):
             words = rows[:].bitcast(F32)
             for u in range(2):
                 nc.tensor.transpose(out=words_t[:, u, :], in_=words[:, u : 2 * P : 2], identity=ident[:])
+
+        def keep_words(words_t):
             nc.vector.tensor_copy(
                 out=xg[:].rearrange("q r c -> q (r c)").bitcast(F32).rearrange("q (r u) -> q r u", u=2),
-                in_=words_t[:, :, 0:used].rearrange("q u r -> q r u"),
+                in_=words_t[:, :, 0:NODES].rearrange("q u r -> q r u"),
             )
-        nc.vector.tensor_copy(out=gain_bias[:], in_=xg[:, NODES:used, :])
+            nc.vector.tensor_copy(out=gain_bias[:], in_=gain_raw[:, :, 0:PACK])
 
         tb = keep.tile([P, GROUPS, P, PACK], BF16, align_bytes=64)
         tb_codes = keep.tile([P, GROUPS, P], U32, align_bytes=64)
         tb_scales = keep.tile([P, GROUPS, P], U8, align_bytes=64)
         nc.gpsimd.memset(tb_scales[:].rearrange("q s m -> q (s m)").bitcast(I32), 0)
-        nc.gpsimd.tensor_scalar(
-            out=tb[:].rearrange("q s (a b) c -> q (s a) b c", b=8),
-            in0=xg[:, 0:NODES, :].unsqueeze(2).to_broadcast([P, NODES, 8, PACK]),
-            scalar1=1.0, scalar2=0.0, op0=ALU.mult, op1=ALU.add,
-        )
+
+        def node_i():
+            nc.vector.tensor_copy(
+                out=tb[:].rearrange("q s (a b) c -> q (s a) b c", b=8),
+                in_=xg[:].unsqueeze(2).to_broadcast([P, NODES, 8, PACK]),
+            )
 
         def node_j(odd, engine_copy):
             part = slice(XP * (1 + odd), XP * (2 + odd))
@@ -105,8 +112,8 @@ def tile_edgeupdaterwrapper_v01_pa_t_kernel(tc, p, x_down, ln_edge_g, ln_edge_b,
                         in_=xg[part, s:NODES:8, :].unsqueeze(1).to_broadcast([XP, 16, 8, PACK]),
                     )
 
-        z_codes = keep.tile([P, QUADS, 2, 2, P], U32, align_bytes=64)
-        z_scales = keep.tile([P, QUADS, 2, 2, P], U8, align_bytes=64)
+        z_codes = keep.tile([P, RING, 2, 2, P], U32, align_bytes=64)
+        z_scales = keep.tile([P, RING, 2, 2, P], U8, align_bytes=64)
 
         def node_operands():
             nc.vector.quantize_mx(
@@ -115,20 +122,21 @@ def tile_edgeupdaterwrapper_v01_pa_t_kernel(tc, p, x_down, ln_edge_g, ln_edge_b,
                 in_=tb[:].rearrange("q s m c -> q (s m c)"),
             )
 
-        def place_i(g):
-            for src, dst in ((tb_codes, z_codes), (tb_scales, z_scales)):
-                nc.sync.dma_start(
-                    out=dst[0:XP, 2 * g : 2 * g + 2].rearrange("q k h r m -> q (k h r) m").bitcast(I32),
-                    in_=src[0:XP, g, :].bitcast(I32).unsqueeze(1).to_broadcast([XP, PER_GROUP, P if src is tb_codes else P // 4]),
+        moves = ((tb_codes, z_codes, P), (tb_scales, z_scales, P // 4))
+
+        def place_i(k, move):
+            for src, dst, words in moves:
+                move(
+                    out=dst[0:XP, k % RING].rearrange("q h r m -> q (h r) m").bitcast(I32),
+                    in_=src[0:XP, k // 2, :].bitcast(I32).unsqueeze(1).to_broadcast([XP, QUAD, words]),
                 )
 
-        def place_j(odd):
-            part = slice(XP * (1 + odd), XP * (2 + odd))
-            for src, dst in ((tb_codes, z_codes), (tb_scales, z_scales)):
-                nc.sync.dma_start(
-                    out=dst[XP : 2 * XP, odd:QUADS:2].rearrange("q k h r m -> q k (h r m)").bitcast(I32),
-                    in_=src[part].rearrange("q s m -> q (s m)").bitcast(I32).unsqueeze(1).to_broadcast(
-                        [XP, GROUPS, QUAD * P if src is tb_codes else QUAD * P // 4]),
+        def place_j(k, move):
+            part = slice(XP * (1 + k % 2), XP * (2 + k % 2))
+            for src, dst, words in moves:
+                move(
+                    out=dst[XP : 2 * XP, k].rearrange("q h r m -> q (h r m)").bitcast(I32),
+                    in_=src[part].rearrange("q s m -> q (s m)").bitcast(I32),
                 )
 
         w_grouped = keep.tile([P, F, PACK], BF16, align_bytes=64)
@@ -165,12 +173,31 @@ def tile_edgeupdaterwrapper_v01_pa_t_kernel(tc, p, x_down, ln_edge_g, ln_edge_b,
             def quad(k):
                 return slice(k * QUAD, (k + 1) * QUAD)
 
+            def on_scalar(t):
+                return t >= 3 * QUAD and t % QUAD >= QUAD - SCALAR_STATS
+
             def sums(t):
-                nc.vector.bn_stats(out=stats[:, t, :], in_=p_sb[:, t, :])
+                if not on_scalar(t):
+                    nc.vector.bn_stats(out=stats[:, t, :], in_=p_sb[:, t, :])
+
+            def sums_on_scalar(t):
+                if on_scalar(t):
+                    unread = work.tile([P, ED], BF16, name="unread")
+                    nc.scalar.activation(
+                        out=unread[:], in_=p_sb[:, t, :], func=ACT.Identity, scale=1.0 / ED, accum_out=mean_var[:, t, 0:1]
+                    )
+                    minus = work.tile([P, 1], F32, name="minus")
+                    nc.scalar.mul(minus[:], mean_var[:, t, 0:1], -(ED ** -0.5))
+                    unread = work.tile([P, ED], BF16, name="unread")
+                    nc.scalar.activation(
+                        out=unread[:], in_=p_sb[:, t, :], func=ACT.Square, bias=minus[:, 0:1], scale=ED ** -0.5,
+                        accum_out=mean_var[:, t, 1:2],
+                    )
 
             def mean_and_variance(k):
                 for t in range(k * QUAD, (k + 1) * QUAD):
-                    nc.vector.bn_aggr(out=mean_var[:, t, :], in_=stats[:, t, :])
+                    if not on_scalar(t):
+                        nc.vector.bn_aggr(out=mean_var[:, t, :], in_=stats[:, t, :])
 
             def scale(k):
                 nc.scalar.activation(
@@ -182,10 +209,16 @@ def tile_edgeupdaterwrapper_v01_pa_t_kernel(tc, p, x_down, ln_edge_g, ln_edge_b,
                     out=shift[:, quad(k)], in0=mean_var[:, quad(k), 0], scalar=-1.0, in1=rstd[:, quad(k)], op0=ALU.mult, op1=ALU.mult
                 )
 
-            def normalise(k, a):
+            def normalise(k, a, on_vector=False):
                 if a == 0:
                     normed_of[k] = work.tile([P, 2, PACK, 2, EP], F32, name="normed")
                 t = k * QUAD + a
+                if on_vector:
+                    nc.vector.tensor_scalar(
+                        out=normed_of[k][:, a // 2, :, a % 2, :], in0=p_sb[:, t, :].rearrange("m (q c) -> m c q", c=PACK),
+                        scalar1=rstd[:, t : t + 1], scalar2=shift[:, t : t + 1], op0=ALU.mult, op1=ALU.add,
+                    )
+                    return
                 nc.scalar.activation(
                     out=normed_of[k][:, a // 2, :, a % 2, :], in_=p_sb[:, t, :].rearrange("m (q c) -> m c q", c=PACK),
                     func=ACT.Identity, bias=shift[:, t : t + 1], scale=rstd[:, t : t + 1],
@@ -202,21 +235,30 @@ def tile_edgeupdaterwrapper_v01_pa_t_kernel(tc, p, x_down, ln_edge_g, ln_edge_b,
                         )
                 turned_of[k] = turned
 
-            def affine(k, c):
+            def affine(k, c, on_vector=False):
                 if c == 0:
                     planes_of[k] = work.tile([P, PACK, 2 * P], BF16, name="planes")
+                if on_vector:
+                    nc.vector.tensor_scalar(
+                        out=planes_of[k][:, c, :], in0=turned_of[k][c // 2][:, c % 2, :, :].rearrange("q r m -> q (r m)"),
+                        scalar1=gain_bias[:, 0, c : c + 1], scalar2=gain_bias[:, 1, c : c + 1], op0=ALU.mult, op1=ALU.add,
+                    )
+                    return
                 nc.scalar.activation(
                     out=planes_of[k][:, c, :], in_=turned_of[k][c // 2][:, c % 2, :, :].rearrange("q r m -> q (r m)"),
                     func=ACT.Identity, bias=gain_bias[:, 1, c : c + 1], scale=gain_bias[:, 0, c : c + 1],
                 )
 
-            def group(k):
+            def group(k, on_vector=False):
                 grouped = work.tile([P, 2 * P, PACK], BF16, align_bytes=64, name="grouped")
+                grouped_of[k] = grouped
+                if on_vector:
+                    nc.vector.tensor_copy(out=grouped[:], in_=planes_of.pop(k)[:].rearrange("q c e -> q e c"))
+                    return
                 nc.gpsimd.tensor_scalar(
                     out=grouped[:], in0=planes_of.pop(k)[:].rearrange("q c e -> q e c"),
                     scalar1=1.0, scalar2=0.0, op0=ALU.mult, op1=ALU.add,
                 )
-                grouped_of[k] = grouped
 
             def quantise(k):
                 nc.vector.quantize_mx(
@@ -229,7 +271,7 @@ def tile_edgeupdaterwrapper_v01_pa_t_kernel(tc, p, x_down, ln_edge_g, ln_edge_b,
                     half = slice(h * EP, (h + 1) * EP)
                     for src, dst in ((u_codes[k % 2], z_codes), (u_scales[k % 2], z_scales)):
                         nc.sync.dma_start(
-                            out=dst[EP:P, k, h].rearrange("q r m -> q (r m)").bitcast(I32), in_=src[half, :].bitcast(I32)
+                            out=dst[EP:P, k % RING, h].rearrange("q r m -> q (r m)").bitcast(I32), in_=src[half, :].bitcast(I32)
                         )
 
             def place_of(t):
@@ -238,10 +280,10 @@ def tile_edgeupdaterwrapper_v01_pa_t_kernel(tc, p, x_down, ln_edge_g, ln_edge_b,
             def multiply(t):
                 k, h, pr = place_of(t)
                 for nh in range(2):
-                    acc = psum_mm.tile([P, N_BANK], F32)
+                    acc = psum_mm.tile([P, N_BANK], F32, name="acc")
                     nc.tensor.matmul_mx(
                         out=acc[:],
-                        lhsT=z_codes[:, k, h, pr, :].bitcast(FP8X4), lhsT_scale=z_scales[:, k, h, pr, :],
+                        lhsT=z_codes[:, k % RING, h, pr, :].bitcast(FP8X4), lhsT_scale=z_scales[:, k % RING, h, pr, :],
                         rhs=w_codes[:, bank(nh)].bitcast(FP8X4), rhs_scale=w_scales[:, bank(nh)],
                         start=True, stop=True,
                     )
@@ -256,9 +298,9 @@ def tile_edgeupdaterwrapper_v01_pa_t_kernel(tc, p, x_down, ln_edge_g, ln_edge_b,
 
             def relu_and_store(t):
                 result = result_of.pop(t)
-                nc.scalar.activation(out=result[:, bank(0)], in_=result[:, bank(0)], func=ACT.Relu)
+                nc.scalar.activation(out=result[:, 0:SCALAR_COLS], in_=result[:, 0:SCALAR_COLS], func=ACT.Relu)
                 nc.gpsimd.tensor_scalar(
-                    out=result[:, bank(1)], in0=result[:, bank(1)],
+                    out=result[:, SCALAR_COLS:F], in0=result[:, SCALAR_COLS:F],
                     scalar1=float("inf"), scalar2=0.0, op0=ALU.min, op1=ALU.max,
                 )
                 nc.sync.dma_start(out=out_view[t // PER_GROUP][:, t % PER_GROUP, :], in_=result[:])
@@ -269,48 +311,107 @@ def tile_edgeupdaterwrapper_v01_pa_t_kernel(tc, p, x_down, ln_edge_g, ln_edge_b,
             def is_tile(t):
                 return 0 <= t < TILES
 
-            for r in range(-3, QUADS + 1):
-                if r == -2:
-                    node_j(0, nc.vector.tensor_copy)
-                    nc.vector.tensor_copy(out=w_grouped[:, bank(0), :], in_=w_raw[:, :, bank(0)].rearrange("q c n -> q n c"))
-                    nc.scalar.copy(out=w_grouped[:, bank(1), :], in_=w_raw[:, :, bank(1)].rearrange("q c n -> q n c"))
-                if r == -1:
-                    node_j(1, nc.vector.tensor_copy)
-                    node_operands()
-                    place_i(0)
-                    place_j(0)
-                    place_j(1)
-                    for g in range(1, GROUPS):
-                        place_i(g)
-                    quantise_weights(0)
-                    quantise_weights(1)
+            def prepare(k):
+                for a in range(QUAD):
+                    sums(k * QUAD + a)
+                mean_and_variance(k)
+                scale(k)
+
+            def move_on_gpsimd(out, in_):
+                nc.gpsimd.tensor_scalar(out=out, in0=in_, scalar1=1.0, scalar2=0.0, op0=ALU.mult, op1=ALU.add)
+
+            prepare(0)
+            words_t = psum_t.tile([P, 2, P], F32, name="turned0")
+            turn_rows(words_t)
+            shift_by_mean(0)
+            for a in range(QUAD):
+                normalise(0, a, on_vector=a % 2 == 1)
+            keep_words(words_t)
+            transpose(0)
+            move_on_gpsimd(w_grouped[:, bank(0), :], w_raw[:, :, bank(0)].rearrange("q c n -> q n c"))
+            node_i()
+            node_j(1, move_on_gpsimd)
+            for a in range(QUAD):
+                sums(QUAD + a)
+            for c in range(PACK):
+                affine(0, c, on_vector=c >= 2)
+            mean_and_variance(1)
+            scale(1)
+            group(0, on_vector=True)
+            shift_by_mean(1)
+            nc.scalar.copy(out=w_grouped[:, bank(1), :], in_=w_raw[:, :, bank(1)].rearrange("q c n -> q n c"))
+            quantise(0)
+            place(0)
+            node_j(0, nc.vector.tensor_copy)
+            node_operands()
+            for a in range(QUAD):
+                normalise(1, a)
+            transpose(1)
+            place_i(0, nc.vector.tensor_copy)
+            place_j(0, nc.vector.tensor_copy)
+            for k in range(1, RING):
+                place_i(k, nc.sync.dma_start)
+                place_j(k, nc.sync.dma_start)
+            quantise_weights(0)
+            quantise_weights(1)
+            for nh in range(2):
+                spread = psum_mm.tile([P, N_BANK], F32, name="acc")
+                nc.tensor.matmul(out=spread[:], lhsT=ones[:], rhs=b1_row[:, bank(nh)], start=True, stop=True)
+                nc.scalar.copy(out=b1_bc[:, bank(nh)], in_=spread[:])
+            for c in range(PACK):
+                affine(1, c)
+            group(1)
+            for a in range(QUAD):
+                sums(2 * QUAD + a)
+            mean_and_variance(2)
+            scale(2)
+
+            for r in range(QUADS + 1):
                 for j in range(QUAD):
                     t = QUAD * r + j
-                    if j == 0 and is_quad(r + 1):
-                        group(r + 1)
+                    if j == 1 and is_quad(r + 2):
+                        transpose(r + 2)
+                    if t == 0:
+                        multiply(0)
+                        multiply(1)
+                    if is_tile(t + 2):
+                        multiply(t + 2)
                     if is_tile(t):
-                        multiply(t)
                         add_bias(t, 0)
-                    if j == 1 and is_quad(r + 1):
-                        quantise(r + 1)
-                        place(r + 1)
+                    if t == 0:
+                        shift_by_mean(2)
+                        quantise(1)
+                        place(1)
+                    if j == 3 and is_quad(r + 2):
+                        quantise(r + 2)
+                        place(r + 2)
+                        if is_quad(r + 4):
+                            place_i(r + 4, nc.sync.dma_start)
                     if j < 2 and is_quad(r + 3):
                         sums(QUAD * (r + 3) + 2 * j)
                         sums(QUAD * (r + 3) + 2 * j + 1)
                     if is_tile(t):
                         add_bias(t, 1)
-                    if j == 2 and is_quad(r + 3):
+                    if j == 1 and is_quad(r + 3):
                         mean_and_variance(r + 3)
-                    if j == 3 and is_quad(r + 3):
-                        scale(r + 3)
-                        shift_by_mean(r + 3)
                     if is_tile(t - 1):
                         relu_and_store(t - 1)
-                    if j < 2 and is_quad(r + 2):
-                        normalise(r + 2, 2 * j)
-                        normalise(r + 2, 2 * j + 1)
-                    if j == 1 and is_quad(r + 2):
-                        transpose(r + 2)
-                    if j >= 2 and is_quad(r + 2):
-                        affine(r + 2, 2 * (j - 2))
-                        affine(r + 2, 2 * (j - 2) + 1)
+                    if t == 0:
+                        for a in range(QUAD):
+                            normalise(2, a)
+                    if j == 0 and is_quad(r + 3):
+                        for a in range(QUAD):
+                            sums_on_scalar(QUAD * (r + 3) + a)
+                    if 1 <= j < 3 and is_quad(r + 2):
+                        affine(r + 2, 2 * j - 2)
+                        affine(r + 2, 2 * j - 1)
+                    if j == 2 and is_quad(r + 2):
+                        group(r + 2)
+                    if j == 2 and is_quad(r + 3):
+                        scale(r + 3)
+                        shift_by_mean(r + 3)
+                        normalise(r + 3, 0)
+                        normalise(r + 3, 1)
+                    if j == 3 and is_quad(r + 3):
+                        normalise(r + 3, 2)
+                        normalise(r + 3, 3)

@@ -24,8 +24,11 @@ N_BANK = 512
 EPS = 1e-5
 QUAD = 4
 QUADS = TILES // QUAD
+SUMS, SCALE, SHIFT, NORM, TURN, AFFINE, GROUP, QUANT = 12, 10, 9, 8, 6, 6, 5, 4
+START = 4
+RELU = 1
 RING = 4
-SCALAR_STATS = 1
+FIRST_ON_SCALAR = 5
 SCALAR_COLS = 384
 XP = HD // PACK
 EP = ED // PACK
@@ -61,9 +64,9 @@ def tile_edgeupdaterwrapper_v01_pa_t_kernel(tc, p, x_down, ln_edge_g, ln_edge_b,
             for h in range(2):
                 nc.sync.dma_start(out=gain_raw[h * EP : (h + 1) * EP, r, 0:PACK], in_=vec.rearrange("(q c) -> q c", c=PACK))
         nc.sync.dma_start(out=w_raw[:, :, 0:N_BANK], in_=w_view[:, :, 0:N_BANK])
+        load_p(QUAD, QUAD)
         nc.sync.dma_start(out=w_raw[:, :, N_BANK:F], in_=w_view[:, :, N_BANK:F])
         nc.sync.dma_start(out=b1_row[0:1, :], in_=b1.rearrange("(o f) -> o f", o=1))
-        load_p(QUAD, QUAD)
         load_p(8, 8)
         load_p(16, 8)
         load_p(24, 8)
@@ -96,10 +99,12 @@ def tile_edgeupdaterwrapper_v01_pa_t_kernel(tc, p, x_down, ln_edge_g, ln_edge_b,
         tb_scales = keep.tile([P, GROUPS, P], U8, align_bytes=64)
         nc.gpsimd.memset(tb_scales[:].rearrange("q s m -> q (s m)").bitcast(I32), 0)
 
+        nc.gpsimd.memset(tb[3 * XP : P, :, :, :].rearrange("q s m c -> q (s m c)").bitcast(I32), 0)
+
         def node_i():
             nc.vector.tensor_copy(
-                out=tb[:].rearrange("q s (a b) c -> q (s a) b c", b=8),
-                in_=xg[:].unsqueeze(2).to_broadcast([P, NODES, 8, PACK]),
+                out=tb[0:XP].rearrange("q s (a b) c -> q (s a) b c", b=8),
+                in_=xg[0:XP].unsqueeze(2).to_broadcast([XP, NODES, 8, PACK]),
             )
 
         def node_j(odd, engine_copy):
@@ -152,8 +157,9 @@ def tile_edgeupdaterwrapper_v01_pa_t_kernel(tc, p, x_down, ln_edge_g, ln_edge_b,
                 in_=w_grouped[:, bank(nh), :].rearrange("q n c -> q (n c)"),
             )
 
-        stats = keep.tile([P, TILES, 6], F32)
-        mean_var = keep.tile([P, TILES, 2], F32)
+        stats = keep.tile([P, TILES // 2, 6], F32)
+        mean = stats[:, :, 1:6:3]
+        square_sum = stats[:, :, 2:6:3]
         rstd = keep.tile([P, TILES], F32)
         shift = keep.tile([P, TILES], F32)
         u_codes = [keep.tile([P, 2 * P], U32, align_bytes=64, name="u_codes%d" % n) for n in range(2)]
@@ -173,40 +179,40 @@ def tile_edgeupdaterwrapper_v01_pa_t_kernel(tc, p, x_down, ln_edge_g, ln_edge_b,
             def quad(k):
                 return slice(k * QUAD, (k + 1) * QUAD)
 
-            def on_scalar(t):
-                return t >= 3 * QUAD and t % QUAD >= QUAD - SCALAR_STATS
+            def on_scalar(pair):
+                return pair % 2 == 1 and pair >= FIRST_ON_SCALAR
 
-            def sums(t):
-                if not on_scalar(t):
-                    nc.vector.bn_stats(out=stats[:, t, :], in_=p_sb[:, t, :])
-
-            def sums_on_scalar(t):
-                if on_scalar(t):
-                    unread = work.tile([P, ED], BF16, name="unread")
-                    nc.scalar.activation(
-                        out=unread[:], in_=p_sb[:, t, :], func=ACT.Identity, scale=1.0 / ED, accum_out=mean_var[:, t, 0:1]
+            def sums(pair):
+                if on_scalar(pair):
+                    for h in range(2):
+                        unread = work.tile([P, ED], BF16, name="unread")
+                        nc.scalar.activation(
+                            out=unread[:], in_=p_sb[:, 2 * pair + h, :], func=ACT.Identity, scale=1.0 / ED,
+                            accum_out=mean[:, pair, h : h + 1],
+                        )
+                        unread = work.tile([P, ED], BF16, name="unread")
+                        nc.scalar.activation(
+                            out=unread[:], in_=p_sb[:, 2 * pair + h, :], func=ACT.Square, bias=mean[:, pair, h : h + 1],
+                            scale=-1.0, accum_out=square_sum[:, pair, h : h + 1],
+                        )
+                else:
+                    nc.vector.bn_stats(
+                        out=stats[:, pair, :], in_=p_sb[:, 2 * pair : 2 * pair + 2, :].rearrange("m h f -> m f h")
                     )
-                    minus = work.tile([P, 1], F32, name="minus")
-                    nc.scalar.mul(minus[:], mean_var[:, t, 0:1], -(ED ** -0.5))
-                    unread = work.tile([P, ED], BF16, name="unread")
-                    nc.scalar.activation(
-                        out=unread[:], in_=p_sb[:, t, :], func=ACT.Square, bias=minus[:, 0:1], scale=ED ** -0.5,
-                        accum_out=mean_var[:, t, 1:2],
-                    )
 
-            def mean_and_variance(k):
-                for t in range(k * QUAD, (k + 1) * QUAD):
-                    if not on_scalar(t):
-                        nc.vector.bn_aggr(out=mean_var[:, t, :], in_=stats[:, t, :])
+            def pairs_of(k):
+                return slice(2 * k, 2 * k + 2)
 
             def scale(k):
                 nc.scalar.activation(
-                    out=rstd[:, quad(k)], in_=mean_var[:, quad(k), 1], func=ACT.Abs_reciprocal_sqrt, bias=eps[:, 0:1], scale=1.0
+                    out=rstd[:, quad(k)].rearrange("m (r h) -> m r h", h=2), in_=square_sum[:, pairs_of(k), :],
+                    func=ACT.Abs_reciprocal_sqrt, bias=eps[:, 0:1], scale=1.0 / ED,
                 )
 
             def shift_by_mean(k):
                 nc.vector.scalar_tensor_tensor(
-                    out=shift[:, quad(k)], in0=mean_var[:, quad(k), 0], scalar=-1.0, in1=rstd[:, quad(k)], op0=ALU.mult, op1=ALU.mult
+                    out=shift[:, quad(k)].rearrange("m (r h) -> m r h", h=2), in0=mean[:, pairs_of(k), :], scalar=-1.0,
+                    in1=rstd[:, quad(k)].rearrange("m (r h) -> m r h", h=2), op0=ALU.mult, op1=ALU.mult,
                 )
 
             def normalise(k, a, on_vector=False):
@@ -311,107 +317,100 @@ def tile_edgeupdaterwrapper_v01_pa_t_kernel(tc, p, x_down, ln_edge_g, ln_edge_b,
             def is_tile(t):
                 return 0 <= t < TILES
 
-            def prepare(k):
-                for a in range(QUAD):
-                    sums(k * QUAD + a)
-                mean_and_variance(k)
-                scale(k)
-
             def move_on_gpsimd(out, in_):
                 nc.gpsimd.tensor_scalar(out=out, in0=in_, scalar1=1.0, scalar2=0.0, op0=ALU.mult, op1=ALU.add)
 
-            prepare(0)
-            words_t = psum_t.tile([P, 2, P], F32, name="turned0")
+            def regroup_weights(nh, move):
+                move(out=w_grouped[:, bank(nh), :], in_=w_raw[:, :, bank(nh)].rearrange("q c n -> q n c"))
+
+            def spread_b1():
+                for nh in range(2):
+                    spread = psum_mm.tile([P, N_BANK], F32, name="acc")
+                    nc.tensor.matmul(out=spread[:], lhsT=ones[:], rhs=b1_row[:, bank(nh)], start=True, stop=True)
+                    nc.scalar.copy(out=b1_bc[:, bank(nh)], in_=spread[:])
+
+            def quad_at(t, lead):
+                k, a = divmod(t + lead, QUAD)
+                return (k, a) if is_quad(k) else (None, None)
+
+            words_t = psum_mm.tile([P, 2, P], F32, name="acc")
             turn_rows(words_t)
+            for pair in range(2):
+                sums(pair)
+            scale(0)
+            keep_words(words_t)
             shift_by_mean(0)
             for a in range(QUAD):
                 normalise(0, a, on_vector=a % 2 == 1)
-            keep_words(words_t)
             transpose(0)
-            move_on_gpsimd(w_grouped[:, bank(0), :], w_raw[:, :, bank(0)].rearrange("q c n -> q n c"))
-            node_i()
-            node_j(1, move_on_gpsimd)
-            for a in range(QUAD):
-                sums(QUAD + a)
+            for nh in range(2):
+                regroup_weights(nh, move_on_gpsimd)
+            node_j(0, nc.scalar.copy)
+            for pair in range(2, 4):
+                sums(pair)
             for c in range(PACK):
                 affine(0, c, on_vector=c >= 2)
-            mean_and_variance(1)
             scale(1)
+            node_j(1, nc.scalar.copy)
             group(0, on_vector=True)
             shift_by_mean(1)
-            nc.scalar.copy(out=w_grouped[:, bank(1), :], in_=w_raw[:, :, bank(1)].rearrange("q c n -> q n c"))
             quantise(0)
             place(0)
-            node_j(0, nc.vector.tensor_copy)
-            node_operands()
+            node_i()
             for a in range(QUAD):
                 normalise(1, a)
-            transpose(1)
+            node_operands()
             place_i(0, nc.vector.tensor_copy)
             place_j(0, nc.vector.tensor_copy)
             for k in range(1, RING):
                 place_i(k, nc.sync.dma_start)
                 place_j(k, nc.sync.dma_start)
+            spread_b1()
             quantise_weights(0)
             quantise_weights(1)
-            for nh in range(2):
-                spread = psum_mm.tile([P, N_BANK], F32, name="acc")
-                nc.tensor.matmul(out=spread[:], lhsT=ones[:], rhs=b1_row[:, bank(nh)], start=True, stop=True)
-                nc.scalar.copy(out=b1_bc[:, bank(nh)], in_=spread[:])
+            transpose(1)
             for c in range(PACK):
                 affine(1, c)
             group(1)
-            for a in range(QUAD):
-                sums(2 * QUAD + a)
-            mean_and_variance(2)
-            scale(2)
 
-            for r in range(QUADS + 1):
-                for j in range(QUAD):
-                    t = QUAD * r + j
-                    if j == 1 and is_quad(r + 2):
-                        transpose(r + 2)
-                    if t == 0:
-                        multiply(0)
-                        multiply(1)
-                    if is_tile(t + 2):
-                        multiply(t + 2)
-                    if is_tile(t):
-                        add_bias(t, 0)
-                    if t == 0:
-                        shift_by_mean(2)
-                        quantise(1)
-                        place(1)
-                    if j == 3 and is_quad(r + 2):
-                        quantise(r + 2)
-                        place(r + 2)
-                        if is_quad(r + 4):
-                            place_i(r + 4, nc.sync.dma_start)
-                    if j < 2 and is_quad(r + 3):
-                        sums(QUAD * (r + 3) + 2 * j)
-                        sums(QUAD * (r + 3) + 2 * j + 1)
-                    if is_tile(t):
-                        add_bias(t, 1)
-                    if j == 1 and is_quad(r + 3):
-                        mean_and_variance(r + 3)
-                    if is_tile(t - 1):
-                        relu_and_store(t - 1)
-                    if t == 0:
-                        for a in range(QUAD):
-                            normalise(2, a)
-                    if j == 0 and is_quad(r + 3):
-                        for a in range(QUAD):
-                            sums_on_scalar(QUAD * (r + 3) + a)
-                    if 1 <= j < 3 and is_quad(r + 2):
-                        affine(r + 2, 2 * j - 2)
-                        affine(r + 2, 2 * j - 1)
-                    if j == 2 and is_quad(r + 2):
-                        group(r + 2)
-                    if j == 2 and is_quad(r + 3):
-                        scale(r + 3)
-                        shift_by_mean(r + 3)
-                        normalise(r + 3, 0)
-                        normalise(r + 3, 1)
-                    if j == 3 and is_quad(r + 3):
-                        normalise(r + 3, 2)
-                        normalise(r + 3, 3)
+            for t in range(-START, TILES + RELU):
+                k, a = quad_at(t, TURN)
+                if k and k > 1 and a == 0:
+                    transpose(k)
+                if is_tile(t + 2):
+                    multiply(t + 2)
+                if is_tile(t):
+                    add_bias(t, 0)
+                if t == 1:
+                    quantise(1)
+                    place(1)
+                k, a = quad_at(t, SUMS)
+                if k and k > 1 and a < 2:
+                    sums(2 * k + a)
+                k, a = quad_at(t, SCALE)
+                if k and k > 1 and a == 0:
+                    scale(k)
+                k, a = quad_at(t, QUANT)
+                if k and k > 1 and a == 0:
+                    quantise(k)
+                    place(k)
+                    if is_quad(k + 2) and k + 2 >= RING:
+                        place_i(k + 2, nc.sync.dma_start)
+                if is_tile(t):
+                    add_bias(t, 1)
+                k, a = quad_at(t, SHIFT)
+                if k and k > 1 and a == 0:
+                    shift_by_mean(k)
+                if is_tile(t - RELU):
+                    relu_and_store(t - RELU)
+                k, a = quad_at(t, NORM)
+                if k and k > 1 and a < 2:
+                    normalise(k, 2 * a)
+                    normalise(k, 2 * a + 1)
+                k, a = quad_at(t, AFFINE)
+                if k and k > 1 and a < 2:
+                    affine(k, 2 * a)
+                    affine(k, 2 * a + 1)
+                k, a = quad_at(t, GROUP)
+                if k and k > 1 and a == 0:
+                    group(k)

@@ -24,11 +24,20 @@ N_BANK = 512
 EPS = 1e-5
 QUAD = 4
 QUADS = TILES // QUAD
-SUMS, SCALE, SHIFT, NORM, TURN, AFFINE, GROUP, QUANT = 12, 10, 9, 8, 6, 6, 5, 4
+LEADS = {"sums": 12, "scale": 10, "shift": 9, "norm": 8, "turn": 6, "affine": 6, "group": 5, "quant": 4}
+LEADS_2 = {"sums": 12, "scale": 10, "shift": 9, "norm": 8, "turn": 6, "affine": 6, "group": 5, "quant": 4}
 START = 4
 RELU = 1
+ON_VECTOR = lambda k: k % 2 == 1
 RING = 4
+TWO_TILES = 2 * (P + P // 4)
 FIRST_ON_SCALAR = 5
+FIRST_PAIR = 8
+STORE = 2
+OUT_BUFS = 5
+GPAIR = 2
+WHOLE = 32
+W_PIECE = 128
 SCALAR_COLS = 384
 XP = HD // PACK
 EP = ED // PACK
@@ -88,16 +97,15 @@ def tile_edgeupdaterwrapper_v01_pa_t_kernel(tc, p, x_down, ln_edge_g, ln_edge_b,
                 nc.tensor.transpose(out=words_t[:, u, :], in_=words[:, u : 2 * P : 2], identity=ident[:])
 
         def keep_words(words_t):
-            nc.vector.tensor_copy(
+            nc.scalar.copy(
                 out=xg[:].rearrange("q r c -> q (r c)").bitcast(F32).rearrange("q (r u) -> q r u", u=2),
                 in_=words_t[:, :, 0:NODES].rearrange("q u r -> q r u"),
             )
-            nc.vector.tensor_copy(out=gain_bias[:], in_=gain_raw[:, :, 0:PACK])
+            nc.scalar.copy(out=gain_bias[:], in_=gain_raw[:, :, 0:PACK])
 
         tb = keep.tile([P, GROUPS, P, PACK], BF16, align_bytes=64)
-        tb_codes = keep.tile([P, GROUPS, P], U32, align_bytes=64)
-        tb_scales = keep.tile([P, GROUPS, P], U8, align_bytes=64)
-        nc.gpsimd.memset(tb_scales[:].rearrange("q s m -> q (s m)").bitcast(I32), 0)
+        tb_packed = keep.tile([P, 2, TWO_TILES], I32, align_bytes=64)
+        nc.gpsimd.memset(tb_packed[:].rearrange("q h w -> q (h w)"), 0)
 
         nc.gpsimd.memset(tb[3 * XP : P, :, :, :].rearrange("q s m c -> q (s m c)").bitcast(I32), 0)
 
@@ -117,32 +125,29 @@ def tile_edgeupdaterwrapper_v01_pa_t_kernel(tc, p, x_down, ln_edge_g, ln_edge_b,
                         in_=xg[part, s:NODES:8, :].unsqueeze(1).to_broadcast([XP, 16, 8, PACK]),
                     )
 
-        z_codes = keep.tile([P, RING, 2, 2, P], U32, align_bytes=64)
-        z_scales = keep.tile([P, RING, 2, 2, P], U8, align_bytes=64)
+        z_packed = keep.tile([P, RING, 2, TWO_TILES], I32, align_bytes=64)
 
         def node_operands():
-            nc.vector.quantize_mx(
-                out=tb_codes[:].rearrange("q s m -> q (s m)").bitcast(FP8X4),
-                scales=tb_scales[:].rearrange("q s m -> q (s m)"),
-                in_=tb[:].rearrange("q s m c -> q (s m c)"),
-            )
-
-        moves = ((tb_codes, z_codes, P), (tb_scales, z_scales, P // 4))
+            for h in range(2):
+                nc.vector.quantize_mx(
+                    out=tb_packed[:, h, 0 : 2 * P].bitcast(FP8X4), scales=tb_packed[:, h, 2 * P : TWO_TILES].bitcast(U8),
+                    in_=tb[:, 2 * h : 2 * h + 2].rearrange("q s m c -> q (s m c)"),
+                )
 
         def place_i(k, move):
-            for src, dst, words in moves:
-                move(
-                    out=dst[0:XP, k % RING].rearrange("q h r m -> q (h r) m").bitcast(I32),
-                    in_=src[0:XP, k // 2, :].bitcast(I32).unsqueeze(1).to_broadcast([XP, QUAD, words]),
-                )
+            h, r = k // 4, k // 2 % 2
+            for start, words in ((0, P), (2 * P, P // 4)):
+                for half in range(2):
+                    move(
+                        out=z_packed[0:XP, k % RING, half, start : start + 2 * words].rearrange("q (r m) -> q r m", r=2),
+                        in_=tb_packed[0:XP, h, start + r * words : start + (r + 1) * words].unsqueeze(1).to_broadcast([XP, 2, words]),
+                    )
 
         def place_j(k, move):
             part = slice(XP * (1 + k % 2), XP * (2 + k % 2))
-            for src, dst, words in moves:
-                move(
-                    out=dst[XP : 2 * XP, k].rearrange("q h r m -> q (h r m)").bitcast(I32),
-                    in_=src[part].rearrange("q s m -> q (s m)").bitcast(I32),
-                )
+            move(
+                out=z_packed[XP : 2 * XP, k].rearrange("q h w -> q (h w)"), in_=tb_packed[part].rearrange("q h w -> q (h w)")
+            )
 
         w_grouped = keep.tile([P, F, PACK], BF16, align_bytes=64)
         w_codes = keep.tile([P, F], U32, align_bytes=64)
@@ -162,12 +167,11 @@ def tile_edgeupdaterwrapper_v01_pa_t_kernel(tc, p, x_down, ln_edge_g, ln_edge_b,
         square_sum = stats[:, :, 2:6:3]
         rstd = keep.tile([P, TILES], F32)
         shift = keep.tile([P, TILES], F32)
-        u_codes = [keep.tile([P, 2 * P], U32, align_bytes=64, name="u_codes%d" % n) for n in range(2)]
-        u_scales = [keep.tile([P, 2 * P], U8, align_bytes=64, name="u_scales%d" % n) for n in range(2)]
+        u_packed = [keep.tile([P, TWO_TILES], I32, align_bytes=64, name="u_packed%d" % n) for n in range(2)]
         for n in range(2):
-            nc.vector.memset(u_scales[n][:].bitcast(I32), 0)
+            nc.gpsimd.memset(u_packed[n][:, 2 * P : TWO_TILES], 0)
 
-        with tc.tile_pool(name="work", bufs=2) as work, tc.tile_pool(name="outs", bufs=8) as outs, \
+        with tc.tile_pool(name="work", bufs=2) as work, tc.tile_pool(name="outs", bufs=OUT_BUFS) as outs, \
                 tc.psum_pool(name="psum_t", bufs=1) as psum_t, tc.psum_pool(name="psum_mm", bufs=6) as psum_mm:
             normed_of = {}
             turned_of = {}
@@ -180,7 +184,7 @@ def tile_edgeupdaterwrapper_v01_pa_t_kernel(tc, p, x_down, ln_edge_g, ln_edge_b,
                 return slice(k * QUAD, (k + 1) * QUAD)
 
             def on_scalar(pair):
-                return pair % 2 == 1 and pair >= FIRST_ON_SCALAR
+                return pair % 2 == 1 and pair >= 5
 
             def sums(pair):
                 if on_scalar(pair):
@@ -215,12 +219,12 @@ def tile_edgeupdaterwrapper_v01_pa_t_kernel(tc, p, x_down, ln_edge_g, ln_edge_b,
                     in1=rstd[:, quad(k)].rearrange("m (r h) -> m r h", h=2), op0=ALU.mult, op1=ALU.mult,
                 )
 
-            def normalise(k, a, on_vector=False):
+            def normalise(k, a, engine=None):
                 if a == 0:
                     normed_of[k] = work.tile([P, 2, PACK, 2, EP], F32, name="normed")
                 t = k * QUAD + a
-                if on_vector:
-                    nc.vector.tensor_scalar(
+                if engine is not None:
+                    engine.tensor_scalar(
                         out=normed_of[k][:, a // 2, :, a % 2, :], in0=p_sb[:, t, :].rearrange("m (q c) -> m c q", c=PACK),
                         scalar1=rstd[:, t : t + 1], scalar2=shift[:, t : t + 1], op0=ALU.mult, op1=ALU.add,
                     )
@@ -267,18 +271,15 @@ def tile_edgeupdaterwrapper_v01_pa_t_kernel(tc, p, x_down, ln_edge_g, ln_edge_b,
                 )
 
             def quantise(k):
+                u = u_packed[k % 2]
                 nc.vector.quantize_mx(
-                    out=u_codes[k % 2][:].bitcast(FP8X4), scales=u_scales[k % 2][:],
+                    out=u[:, 0 : 2 * P].bitcast(FP8X4), scales=u[:, 2 * P : TWO_TILES].bitcast(U8),
                     in_=grouped_of.pop(k)[:].rearrange("q e c -> q (e c)"),
                 )
 
             def place(k):
                 for h in range(2):
-                    half = slice(h * EP, (h + 1) * EP)
-                    for src, dst in ((u_codes[k % 2], z_codes), (u_scales[k % 2], z_scales)):
-                        nc.sync.dma_start(
-                            out=dst[EP:P, k % RING, h].rearrange("q r m -> q (r m)").bitcast(I32), in_=src[half, :].bitcast(I32)
-                        )
+                    (nc.vector.tensor_copy if h == 1 and ON_VECTOR(k) else nc.sync.dma_start)(out=z_packed[EP:P, k % RING, h, :], in_=u_packed[k % 2][h * EP : (h + 1) * EP, :])
 
             def place_of(t):
                 return t // QUAD, t % 2, (t % QUAD) // 2
@@ -289,27 +290,36 @@ def tile_edgeupdaterwrapper_v01_pa_t_kernel(tc, p, x_down, ln_edge_g, ln_edge_b,
                     acc = psum_mm.tile([P, N_BANK], F32, name="acc")
                     nc.tensor.matmul_mx(
                         out=acc[:],
-                        lhsT=z_codes[:, k % RING, h, pr, :].bitcast(FP8X4), lhsT_scale=z_scales[:, k % RING, h, pr, :],
+                        lhsT=z_packed[:, k % RING, h, pr * P : (pr + 1) * P].bitcast(FP8X4),
+                        lhsT_scale=z_packed[:, k % RING, h, 2 * P + pr * P // 4 : 2 * P + (pr + 1) * P // 4].bitcast(U8),
                         rhs=w_codes[:, bank(nh)].bitcast(FP8X4), rhs_scale=w_scales[:, bank(nh)],
                         start=True, stop=True,
                     )
                     acc_of[(t, nh)] = acc
 
             def add_bias(t, nh):
-                if nh == 0:
-                    result_of[t] = outs.tile([P, F], F32, name="result")
+                if nh == 0 and t % STORE == 0:
+                    result_of[t // STORE] = outs.tile([P, STORE, F], F32, name="result")
                 nc.vector.tensor_tensor(
-                    out=result_of[t][:, bank(nh)], in0=acc_of.pop((t, nh))[:], in1=b1_bc[:, bank(nh)], op=ALU.add
+                    out=result_of[t // STORE][:, t % STORE, bank(nh)], in0=acc_of.pop((t, nh))[:], in1=b1_bc[:, bank(nh)], op=ALU.add
                 )
 
             def relu_and_store(t):
-                result = result_of.pop(t)
-                nc.scalar.activation(out=result[:, 0:SCALAR_COLS], in_=result[:, 0:SCALAR_COLS], func=ACT.Relu)
-                nc.gpsimd.tensor_scalar(
-                    out=result[:, SCALAR_COLS:F], in0=result[:, SCALAR_COLS:F],
-                    scalar1=float("inf"), scalar2=0.0, op0=ALU.min, op1=ALU.max,
-                )
-                nc.sync.dma_start(out=out_view[t // PER_GROUP][:, t % PER_GROUP, :], in_=result[:])
+                a = t % STORE
+                result = result_of[t // STORE]
+                nc.scalar.activation(out=result[:, a, 0:SCALAR_COLS], in_=result[:, a, 0:SCALAR_COLS], func=ACT.Relu)
+                if not FIRST_PAIR <= t < WHOLE or a % GPAIR == GPAIR - 1:
+                    b = a - GPAIR + 1 if FIRST_PAIR <= t < WHOLE else a
+                    nc.gpsimd.tensor_scalar(
+                        out=result[:, b : a + 1, SCALAR_COLS:F], in0=result[:, b : a + 1, SCALAR_COLS:F],
+                        scalar1=1.0, scalar2=0.0, op0=ALU.mult, op1=ALU.max,
+                    )
+                g, first = t // PER_GROUP, t % PER_GROUP - a
+                if FIRST_PAIR <= t < WHOLE:
+                    if a == STORE - 1:
+                        nc.sync.dma_start(out=out_view[g][:, first : first + STORE, :], in_=result[:])
+                else:
+                    nc.sync.dma_start(out=out_view[g][:, first + a, :], in_=result[:, a, :])
 
             def is_quad(k):
                 return 0 <= k < QUADS
@@ -320,8 +330,9 @@ def tile_edgeupdaterwrapper_v01_pa_t_kernel(tc, p, x_down, ln_edge_g, ln_edge_b,
             def move_on_gpsimd(out, in_):
                 nc.gpsimd.tensor_scalar(out=out, in0=in_, scalar1=1.0, scalar2=0.0, op0=ALU.mult, op1=ALU.add)
 
-            def regroup_weights(nh, move):
-                move(out=w_grouped[:, bank(nh), :], in_=w_raw[:, :, bank(nh)].rearrange("q c n -> q n c"))
+            def regroup_weights(piece, move):
+                cols = slice(piece * W_PIECE, (piece + 1) * W_PIECE)
+                move(out=w_grouped[:, cols, :], in_=w_raw[:, :, cols].rearrange("q c n -> q n c"))
 
             def spread_b1():
                 for nh in range(2):
@@ -329,9 +340,13 @@ def tile_edgeupdaterwrapper_v01_pa_t_kernel(tc, p, x_down, ln_edge_g, ln_edge_b,
                     nc.tensor.matmul(out=spread[:], lhsT=ones[:], rhs=b1_row[:, bank(nh)], start=True, stop=True)
                     nc.scalar.copy(out=b1_bc[:, bank(nh)], in_=spread[:])
 
-            def quad_at(t, lead):
-                k, a = divmod(t + lead, QUAD)
-                return (k, a) if is_quad(k) else (None, None)
+            def at(stage, t):
+                found = []
+                for k in range(2, QUADS):
+                    a = t - QUAD * k + (LEADS_2 if k == 2 else LEADS)[stage]
+                    if 0 <= a < QUAD:
+                        found.append((k, a))
+                return found
 
             words_t = psum_mm.tile([P, 2, P], F32, name="acc")
             turn_rows(words_t)
@@ -341,10 +356,10 @@ def tile_edgeupdaterwrapper_v01_pa_t_kernel(tc, p, x_down, ln_edge_g, ln_edge_b,
             keep_words(words_t)
             shift_by_mean(0)
             for a in range(QUAD):
-                normalise(0, a, on_vector=a % 2 == 1)
+                normalise(0, a, nc.vector if a % 2 == 1 else None)
             transpose(0)
-            for nh in range(2):
-                regroup_weights(nh, move_on_gpsimd)
+            for piece in range(F // W_PIECE):
+                regroup_weights(piece, move_on_gpsimd)
             node_j(0, nc.scalar.copy)
             for pair in range(2, 4):
                 sums(pair)
@@ -374,8 +389,7 @@ def tile_edgeupdaterwrapper_v01_pa_t_kernel(tc, p, x_down, ln_edge_g, ln_edge_b,
             group(1)
 
             for t in range(-START, TILES + RELU):
-                k, a = quad_at(t, TURN)
-                if k and k > 1 and a == 0:
+                for k, a in [x for x in at("turn", t) if x[1] < 1]:
                     transpose(k)
                 if is_tile(t + 2):
                     multiply(t + 2)
@@ -384,33 +398,26 @@ def tile_edgeupdaterwrapper_v01_pa_t_kernel(tc, p, x_down, ln_edge_g, ln_edge_b,
                 if t == 1:
                     quantise(1)
                     place(1)
-                k, a = quad_at(t, SUMS)
-                if k and k > 1 and a < 2:
+                for k, a in [x for x in at("sums", t) if x[1] < 2]:
                     sums(2 * k + a)
-                k, a = quad_at(t, SCALE)
-                if k and k > 1 and a == 0:
+                for k, a in [x for x in at("scale", t) if x[1] < 1]:
                     scale(k)
-                k, a = quad_at(t, QUANT)
-                if k and k > 1 and a == 0:
+                for k, a in [x for x in at("quant", t) if x[1] < 1]:
                     quantise(k)
                     place(k)
                     if is_quad(k + 2) and k + 2 >= RING:
                         place_i(k + 2, nc.sync.dma_start)
                 if is_tile(t):
                     add_bias(t, 1)
-                k, a = quad_at(t, SHIFT)
-                if k and k > 1 and a == 0:
+                for k, a in [x for x in at("shift", t) if x[1] < 1]:
                     shift_by_mean(k)
                 if is_tile(t - RELU):
                     relu_and_store(t - RELU)
-                k, a = quad_at(t, NORM)
-                if k and k > 1 and a < 2:
+                for k, a in [x for x in at("norm", t) if x[1] < 2]:
                     normalise(k, 2 * a)
                     normalise(k, 2 * a + 1)
-                k, a = quad_at(t, AFFINE)
-                if k and k > 1 and a < 2:
+                for k, a in [x for x in at("affine", t) if x[1] < 2]:
                     affine(k, 2 * a)
                     affine(k, 2 * a + 1)
-                k, a = quad_at(t, GROUP)
-                if k and k > 1 and a == 0:
+                for k, a in [x for x in at("group", t) if x[1] < 1]:
                     group(k)

@@ -312,7 +312,7 @@ def tile_edgeupdaterwrapper_v01_pa_t_kernel(tc, p, x_down, ln_edge_g, ln_edge_b,
                     b = a - GPAIR + 1 if FIRST_PAIR <= t < WHOLE else a
                     nc.gpsimd.tensor_scalar(
                         out=result[:, b : a + 1, SCALAR_COLS:F], in0=result[:, b : a + 1, SCALAR_COLS:F],
-                        scalar1=1.0, scalar2=0.0, op0=ALU.mult, op1=ALU.max,
+                        scalar1=float("inf"), scalar2=0.0, op0=ALU.min, op1=ALU.max,
                     )
                 g, first = t // PER_GROUP, t % PER_GROUP - a
                 if FIRST_PAIR <= t < WHOLE:

@@ -28,17 +28,16 @@ LEADS = {"sums": 12, "scale": 10, "shift": 9, "norm": 8, "turn": 6, "affine": 6,
 LEADS_2 = {"sums": 12, "scale": 10, "shift": 9, "norm": 8, "turn": 6, "affine": 6, "group": 5, "quant": 4}
 START = 4
 RELU = 1
-ON_VECTOR = lambda k: k % 2 == 1
 RING = 4
 TWO_TILES = 2 * (P + P // 4)
 FIRST_ON_SCALAR = 5
 FIRST_PAIR = 8
 STORE = 2
 OUT_BUFS = 5
-GPAIR = 2
+GPAIR = 1
 WHOLE = 32
 W_PIECE = 128
-SCALAR_COLS = 384
+SCALAR_COLS = 320
 XP = HD // PACK
 EP = ED // PACK
 
@@ -279,7 +278,7 @@ def tile_edgeupdaterwrapper_v01_pa_t_kernel(tc, p, x_down, ln_edge_g, ln_edge_b,
 
             def place(k):
                 for h in range(2):
-                    (nc.vector.tensor_copy if h == 1 and ON_VECTOR(k) else nc.sync.dma_start)(out=z_packed[EP:P, k % RING, h, :], in_=u_packed[k % 2][h * EP : (h + 1) * EP, :])
+                    nc.sync.dma_start(out=z_packed[EP:P, k % RING, h, :], in_=u_packed[k % 2][h * EP : (h + 1) * EP, :])
 
             def place_of(t):
                 return t // QUAD, t % 2, (t % QUAD) // 2

@@ -28,6 +28,15 @@ LEADS = {"sums": 12, "scale": 10, "shift": 9, "norm": 8, "turn": 6, "affine": 6,
 LEADS_2 = {"sums": 12, "scale": 10, "shift": 9, "norm": 8, "turn": 6, "affine": 6, "group": 5, "quant": 4}
 START = 4
 RELU = 1
+NJ1 = 0
+GV = lambda k: k >= 6
+LATE = 24
+LATE_COLS = 512
+N1G = 0
+N2G = 0
+EARLY2 = 1
+X0V = 1
+RULE = lambda pair: pair % 2 == 1 and pair >= 5
 RING = 4
 TWO_TILES = 2 * (P + P // 4)
 FIRST_ON_SCALAR = 5
@@ -36,8 +45,8 @@ STORE = 2
 OUT_BUFS = 5
 GPAIR = 1
 WHOLE = 32
-W_PIECE = 128
-SCALAR_COLS = 320
+W_PIECE = 256
+SCALAR_COLS = 384
 XP = HD // PACK
 EP = ED // PACK
 
@@ -104,9 +113,9 @@ def tile_edgeupdaterwrapper_v01_pa_t_kernel(tc, p, x_down, ln_edge_g, ln_edge_b,
 
         tb = keep.tile([P, GROUPS, P, PACK], BF16, align_bytes=64)
         tb_packed = keep.tile([P, 2, TWO_TILES], I32, align_bytes=64)
-        nc.gpsimd.memset(tb_packed[:].rearrange("q h w -> q (h w)"), 0)
+        nc.vector.memset(tb_packed[:, :, 2 * P : TWO_TILES], 0)
 
-        nc.gpsimd.memset(tb[3 * XP : P, :, :, :].rearrange("q s m c -> q (s m c)").bitcast(I32), 0)
+        nc.vector.memset(tb[3 * XP : P, :, :, :].rearrange("q s m c -> q (s m c)").bitcast(I32), 0)
 
         def node_i():
             nc.vector.tensor_copy(
@@ -168,7 +177,7 @@ def tile_edgeupdaterwrapper_v01_pa_t_kernel(tc, p, x_down, ln_edge_g, ln_edge_b,
         shift = keep.tile([P, TILES], F32)
         u_packed = [keep.tile([P, TWO_TILES], I32, align_bytes=64, name="u_packed%d" % n) for n in range(2)]
         for n in range(2):
-            nc.gpsimd.memset(u_packed[n][:, 2 * P : TWO_TILES], 0)
+            nc.vector.memset(u_packed[n][:, 2 * P : TWO_TILES], 0)
 
         with tc.tile_pool(name="work", bufs=2) as work, tc.tile_pool(name="outs", bufs=OUT_BUFS) as outs, \
                 tc.psum_pool(name="psum_t", bufs=1) as psum_t, tc.psum_pool(name="psum_mm", bufs=6) as psum_mm:
@@ -183,7 +192,7 @@ def tile_edgeupdaterwrapper_v01_pa_t_kernel(tc, p, x_down, ln_edge_g, ln_edge_b,
                 return slice(k * QUAD, (k + 1) * QUAD)
 
             def on_scalar(pair):
-                return pair % 2 == 1 and pair >= 5
+                return RULE(pair)
 
             def sums(pair):
                 if on_scalar(pair):
@@ -304,13 +313,14 @@ def tile_edgeupdaterwrapper_v01_pa_t_kernel(tc, p, x_down, ln_edge_g, ln_edge_b,
                 )
 
             def relu_and_store(t):
+                split = SCALAR_COLS if t < LATE else LATE_COLS
                 a = t % STORE
                 result = result_of[t // STORE]
-                nc.scalar.activation(out=result[:, a, 0:SCALAR_COLS], in_=result[:, a, 0:SCALAR_COLS], func=ACT.Relu)
+                nc.scalar.activation(out=result[:, a, 0:split], in_=result[:, a, 0:split], func=ACT.Relu)
                 if not FIRST_PAIR <= t < WHOLE or a % GPAIR == GPAIR - 1:
                     b = a - GPAIR + 1 if FIRST_PAIR <= t < WHOLE else a
                     nc.gpsimd.tensor_scalar(
-                        out=result[:, b : a + 1, SCALAR_COLS:F], in0=result[:, b : a + 1, SCALAR_COLS:F],
+                        out=result[:, b : a + 1, split:F], in0=result[:, b : a + 1, split:F],
                         scalar1=float("inf"), scalar2=0.0, op0=ALU.min, op1=ALU.max,
                     )
                 g, first = t // PER_GROUP, t % PER_GROUP - a
@@ -357,26 +367,36 @@ def tile_edgeupdaterwrapper_v01_pa_t_kernel(tc, p, x_down, ln_edge_g, ln_edge_b,
             for a in range(QUAD):
                 normalise(0, a, nc.vector if a % 2 == 1 else None)
             transpose(0)
+            if NJ1 == 1:
+                node_j(1, move_on_gpsimd)
             for piece in range(F // W_PIECE):
                 regroup_weights(piece, move_on_gpsimd)
+            if NJ1 == 2:
+                node_j(1, move_on_gpsimd)
             node_j(0, nc.scalar.copy)
             for pair in range(2, 4):
                 sums(pair)
             for c in range(PACK):
                 affine(0, c, on_vector=c >= 2)
             scale(1)
-            node_j(1, nc.scalar.copy)
+            if NJ1 == 0:
+                node_j(1, nc.scalar.copy)
             group(0, on_vector=True)
             shift_by_mean(1)
             quantise(0)
             place(0)
+            if EARLY2:
+                sums(4)
             node_i()
+            if EARLY2:
+                sums(5)
             for a in range(QUAD):
-                normalise(1, a)
+                normalise(1, a, nc.gpsimd if a < N1G else None)
             node_operands()
-            place_i(0, nc.vector.tensor_copy)
-            place_j(0, nc.vector.tensor_copy)
-            for k in range(1, RING):
+            if X0V:
+                place_i(0, nc.vector.tensor_copy)
+                place_j(0, nc.vector.tensor_copy)
+            for k in range(1 if X0V else 0, RING):
                 place_i(k, nc.sync.dma_start)
                 place_j(k, nc.sync.dma_start)
             spread_b1()
@@ -398,7 +418,8 @@ def tile_edgeupdaterwrapper_v01_pa_t_kernel(tc, p, x_down, ln_edge_g, ln_edge_b,
                     quantise(1)
                     place(1)
                 for k, a in [x for x in at("sums", t) if x[1] < 2]:
-                    sums(2 * k + a)
+                    if not (EARLY2 and k == 2):
+                        sums(2 * k + a)
                 for k, a in [x for x in at("scale", t) if x[1] < 1]:
                     scale(k)
                 for k, a in [x for x in at("quant", t) if x[1] < 1]:
@@ -413,10 +434,10 @@ def tile_edgeupdaterwrapper_v01_pa_t_kernel(tc, p, x_down, ln_edge_g, ln_edge_b,
                 if is_tile(t - RELU):
                     relu_and_store(t - RELU)
                 for k, a in [x for x in at("norm", t) if x[1] < 2]:
-                    normalise(k, 2 * a)
-                    normalise(k, 2 * a + 1)
+                    normalise(k, 2 * a, nc.gpsimd if k == 2 and N2G > 1 else None)
+                    normalise(k, 2 * a + 1, nc.gpsimd if k == 2 and N2G > 0 else None)
                 for k, a in [x for x in at("affine", t) if x[1] < 2]:
                     affine(k, 2 * a)
                     affine(k, 2 * a + 1)
                 for k, a in [x for x in at("group", t) if x[1] < 1]:
-                    group(k)
+                    group(k, on_vector=GV(k))

@@ -24,18 +24,20 @@ N_BANK = 512
 EPS = 1e-5
 QUAD = 4
 QUADS = TILES // QUAD
-LEADS = {"sums": 12, "scale": 10, "shift": 9, "norm": 8, "turn": 6, "affine": 6, "group": 5, "quant": 4}
+LEADS = {"sums": 13, "scale": 11, "shift": 10, "norm": 9, "turn": 7, "affine": 7, "group": 6, "quant": 5}
 LEADS_2 = {"sums": 12, "scale": 10, "shift": 9, "norm": 8, "turn": 6, "affine": 6, "group": 5, "quant": 4}
 START = 4
 RELU = 1
 NJ1 = 0
+OV = lambda k: False
+GP2 = 0
 GV = lambda k: k >= 6
 LATE = 24
 LATE_COLS = 512
 N1G = 0
 N2G = 0
-EARLY2 = 1
-X0V = 1
+EARLY2 = 0
+X0V = 0
 RULE = lambda pair: pair % 2 == 1 and pair >= 5
 RING = 4
 TWO_TILES = 2 * (P + P // 4)
@@ -287,7 +289,7 @@ def tile_edgeupdaterwrapper_v01_pa_t_kernel(tc, p, x_down, ln_edge_g, ln_edge_b,
 
             def place(k):
                 for h in range(2):
-                    nc.sync.dma_start(out=z_packed[EP:P, k % RING, h, :], in_=u_packed[k % 2][h * EP : (h + 1) * EP, :])
+                    (nc.vector.tensor_copy if h == 1 and OV(k) else nc.sync.dma_start)(out=z_packed[EP:P, k % RING, h, :], in_=u_packed[k % 2][h * EP : (h + 1) * EP, :])
 
             def place_of(t):
                 return t // QUAD, t % 2, (t % QUAD) // 2
@@ -316,11 +318,20 @@ def tile_edgeupdaterwrapper_v01_pa_t_kernel(tc, p, x_down, ln_edge_g, ln_edge_b,
                 split = SCALAR_COLS if t < LATE else LATE_COLS
                 a = t % STORE
                 result = result_of[t // STORE]
-                nc.scalar.activation(out=result[:, a, 0:split], in_=result[:, a, 0:split], func=ACT.Relu)
-                if not FIRST_PAIR <= t < WHOLE or a % GPAIR == GPAIR - 1:
-                    b = a - GPAIR + 1 if FIRST_PAIR <= t < WHOLE else a
+                paired = FIRST_PAIR <= t < WHOLE
+                if paired and GP2 and a == 1:
+                    nc.scalar.activation(out=result[:, a, F - split : F], in_=result[:, a, F - split : F], func=ACT.Relu)
+                else:
+                    nc.scalar.activation(out=result[:, a, 0:split], in_=result[:, a, 0:split], func=ACT.Relu)
+                if paired and GP2:
+                    if a == 1:
+                        both = result[:].rearrange("m a f -> m (a f)")[:, split : 2 * F - split]
+                        nc.gpsimd.tensor_scalar(
+                            out=both, in0=both, scalar1=float("inf"), scalar2=0.0, op0=ALU.min, op1=ALU.max,
+                        )
+                else:
                     nc.gpsimd.tensor_scalar(
-                        out=result[:, b : a + 1, split:F], in0=result[:, b : a + 1, split:F],
+                        out=result[:, a, split:F], in0=result[:, a, split:F],
                         scalar1=float("inf"), scalar2=0.0, op0=ALU.min, op1=ALU.max,
                     )
                 g, first = t // PER_GROUP, t % PER_GROUP - a

import concourse.mybir as mybir
from concourse.masks import make_identity

F32 = mybir.dt.float32
BF16 = mybir.dt.bfloat16
I32 = mybir.dt.int32
U32 = mybir.dt.uint32
U8 = mybir.dt.uint8
FP8X4 = mybir.dt.float8_e4m3fn_x4
ALU = mybir.AluOpType
ACT = mybir.ActivationFunctionType

P = 128
PACK = 4
NODES = 64
HD = 128
ED = 256
F = 1024
EDGES = NODES * NODES
TILES = EDGES // P
GROUPS = 4
PER_GROUP = TILES // GROUPS
N_BANK = 512
EPS = 1e-5
QUAD = 4
QUADS = TILES // QUAD
LEADS = {"sums": 13, "scale": 11, "shift": 10, "norm": 9, "turn": 7, "affine": 7, "group": 6, "quant": 5}
LEADS_2 = {"sums": 12, "scale": 10, "shift": 9, "norm": 8, "turn": 6, "affine": 6, "group": 5, "quant": 4}
START = 4
RELU = 1
NJ1 = 0
OV = lambda k: False
GP2 = 0
GV = lambda k: k >= 6
LATE = 24
LATE_COLS = 512
N1G = 0
N2G = 0
EARLY2 = 0
X0V = 0
RULE = lambda pair: pair % 2 == 1 and pair >= 5
RING = 4
TWO_TILES = 2 * (P + P // 4)
FIRST_ON_SCALAR = 5
FIRST_PAIR = 8
STORE = 2
OUT_BUFS = 5
GPAIR = 1
WHOLE = 32
W_PIECE = 256
SCALAR_COLS = 384
XP = HD // PACK
EP = ED // PACK

FLOPS = 2 * EDGES * (2 * HD + ED) * F


def tile_edgeupdaterwrapper_v01_pa_t_kernel(tc, p, x_down, ln_edge_g, ln_edge_b, W1, b1, out):
    nc = tc.nc
    p_view = p.rearrange("b i j f -> (b i j) f").rearrange("(g m s) f -> g m s f", g=GROUPS, s=PER_GROUP)
    out_view = out.rearrange("b i j f -> (b i j) f").rearrange("(g m s) f -> g m s f", g=GROUPS, s=PER_GROUP)

    with tc.manual_schedule(), tc.tile_pool(name="keep", bufs=1) as keep:
        p_sb = keep.tile([P, TILES, ED], BF16)
        w_view = W1.rearrange("(q c) n -> q c n", c=PACK)
        w_raw = keep.tile([P, PACK, F], BF16)
        rows = keep.tile([P, 4 * HD], BF16)
        gain_raw = keep.tile([P, 2, 16], BF16)
        b1_row = keep.tile([P, F], BF16)

        def load_p(t0, n):
            g, s = t0 // PER_GROUP, t0 % PER_GROUP
            nc.sync.dma_start(out=p_sb[:, t0 : t0 + n, :], in_=p_view[g][:, s : s + n, :])

        nc.vector.memset(rows[NODES:P, :], 0.0)
        nc.gpsimd.memset(b1_row[:].bitcast(I32), 0)
        load_p(0, QUAD)
        nc.sync.dma_start(
            out=rows[0:NODES, :].rearrange("n (r f) -> n r f", r=4),
            in_=x_down.rearrange("b n f -> (b n) f").unsqueeze(1).to_broadcast([NODES, 4, HD]),
        )
        for r, vec in ((0, ln_edge_g), (1, ln_edge_b)):
            for h in range(2):
                nc.sync.dma_start(out=gain_raw[h * EP : (h + 1) * EP, r, 0:PACK], in_=vec.rearrange("(q c) -> q c", c=PACK))
        nc.sync.dma_start(out=w_raw[:, :, 0:N_BANK], in_=w_view[:, :, 0:N_BANK])
        load_p(QUAD, QUAD)
        nc.sync.dma_start(out=w_raw[:, :, N_BANK:F], in_=w_view[:, :, N_BANK:F])
        nc.sync.dma_start(out=b1_row[0:1, :], in_=b1.rearrange("(o f) -> o f", o=1))
        load_p(8, 8)
        load_p(16, 8)
        load_p(24, 8)

        ident = keep.tile([P, P], F32)
        make_identity(nc, ident[:])
        eps = keep.tile([P, 1], F32)
        nc.vector.memset(eps[:], EPS)
        ones = keep.tile([P, P], BF16)
        nc.vector.memset(ones[:], 1.0)
        b1_bc = keep.tile([P, F], BF16)

        xg = keep.tile([P, NODES, PACK], BF16)
        gain_bias = keep.tile([P, 2, PACK], F32)

        def turn_rows(words_t):
            words = rows[:].bitcast(F32)
            for u in range(2):
                nc.tensor.transpose(out=words_t[:, u, :], in_=words[:, u : 2 * P : 2], identity=ident[:])

        def keep_words(words_t):
            nc.scalar.copy(
                out=xg[:].rearrange("q r c -> q (r c)").bitcast(F32).rearrange("q (r u) -> q r u", u=2),
                in_=words_t[:, :, 0:NODES].rearrange("q u r -> q r u"),
            )
            nc.scalar.copy(out=gain_bias[:], in_=gain_raw[:, :, 0:PACK])

        tb = keep.tile([P, GROUPS, P, PACK], BF16, align_bytes=64)
        tb_packed = keep.tile([P, 2, TWO_TILES], I32, align_bytes=64)
        nc.vector.memset(tb_packed[:, :, 2 * P : TWO_TILES], 0)

        nc.vector.memset(tb[3 * XP : P, :, :, :].rearrange("q s m c -> q (s m c)").bitcast(I32), 0)

        def node_i():
            nc.vector.tensor_copy(
                out=tb[0:XP].rearrange("q s (a b) c -> q (s a) b c", b=8),
                in_=xg[0:XP].unsqueeze(2).to_broadcast([XP, NODES, 8, PACK]),
            )

        def node_j(odd, engine_copy):
            part = slice(XP * (1 + odd), XP * (2 + odd))
            for h in range(2):
                for pr in range(2):
                    s = QUAD * odd + 2 * pr + h
                    engine_copy(
                        out=tb[part, 2 * h + pr, :, :].rearrange("q (a b) c -> q a b c", b=8),
                        in_=xg[part, s:NODES:8, :].unsqueeze(1).to_broadcast([XP, 16, 8, PACK]),
                    )

        z_packed = keep.tile([P, RING, 2, TWO_TILES], I32, align_bytes=64)

        def node_operands():
            for h in range(2):
                nc.vector.quantize_mx(
                    out=tb_packed[:, h, 0 : 2 * P].bitcast(FP8X4), scales=tb_packed[:, h, 2 * P : TWO_TILES].bitcast(U8),
                    in_=tb[:, 2 * h : 2 * h + 2].rearrange("q s m c -> q (s m c)"),
                )

        def place_i(k, move):
            h, r = k // 4, k // 2 % 2
            for start, words in ((0, P), (2 * P, P // 4)):
                for half in range(2):
                    move(
                        out=z_packed[0:XP, k % RING, half, start : start + 2 * words].rearrange("q (r m) -> q r m", r=2),
                        in_=tb_packed[0:XP, h, start + r * words : start + (r + 1) * words].unsqueeze(1).to_broadcast([XP, 2, words]),
                    )

        def place_j(k, move):
            part = slice(XP * (1 + k % 2), XP * (2 + k % 2))
            move(
                out=z_packed[XP : 2 * XP, k].rearrange("q h w -> q (h w)"), in_=tb_packed[part].rearrange("q h w -> q (h w)")
            )

        w_grouped = keep.tile([P, F, PACK], BF16, align_bytes=64)
        w_codes = keep.tile([P, F], U32, align_bytes=64)
        w_scales = keep.tile([P, F], U8, align_bytes=64)

        def bank(nh):
            return slice(nh * N_BANK, (nh + 1) * N_BANK)

        def quantise_weights(nh):
            nc.vector.quantize_mx(
                out=w_codes[:, bank(nh)].bitcast(FP8X4), scales=w_scales[:, bank(nh)],
                in_=w_grouped[:, bank(nh), :].rearrange("q n c -> q (n c)"),
            )

        stats = keep.tile([P, TILES // 2, 6], F32)
        mean = stats[:, :, 1:6:3]
        square_sum = stats[:, :, 2:6:3]
        rstd = keep.tile([P, TILES], F32)
        shift = keep.tile([P, TILES], F32)
        u_packed = [keep.tile([P, TWO_TILES], I32, align_bytes=64, name="u_packed%d" % n) for n in range(2)]
        for n in range(2):
            nc.vector.memset(u_packed[n][:, 2 * P : TWO_TILES], 0)

        with tc.tile_pool(name="work", bufs=2) as work, tc.tile_pool(name="outs", bufs=OUT_BUFS) as outs, \
                tc.psum_pool(name="psum_t", bufs=1) as psum_t, tc.psum_pool(name="psum_mm", bufs=6) as psum_mm:
            normed_of = {}
            turned_of = {}
            planes_of = {}
            grouped_of = {}
            acc_of = {}
            result_of = {}

            def quad(k):
                return slice(k * QUAD, (k + 1) * QUAD)

            def on_scalar(pair):
                return RULE(pair)

            def sums(pair):
                if on_scalar(pair):
                    for h in range(2):
                        unread = work.tile([P, ED], BF16, name="unread")
                        nc.scalar.activation(
                            out=unread[:], in_=p_sb[:, 2 * pair + h, :], func=ACT.Identity, scale=1.0 / ED,
                            accum_out=mean[:, pair, h : h + 1],
                        )
                        unread = work.tile([P, ED], BF16, name="unread")
                        nc.scalar.activation(
                            out=unread[:], in_=p_sb[:, 2 * pair + h, :], func=ACT.Square, bias=mean[:, pair, h : h + 1],
                            scale=-1.0, accum_out=square_sum[:, pair, h : h + 1],
                        )
                else:
                    nc.vector.bn_stats(
                        out=stats[:, pair, :], in_=p_sb[:, 2 * pair : 2 * pair + 2, :].rearrange("m h f -> m f h")
                    )

            def pairs_of(k):
                return slice(2 * k, 2 * k + 2)

            def scale(k):
                nc.scalar.activation(
                    out=rstd[:, quad(k)].rearrange("m (r h) -> m r h", h=2), in_=square_sum[:, pairs_of(k), :],
                    func=ACT.Abs_reciprocal_sqrt, bias=eps[:, 0:1], scale=1.0 / ED,
                )

            def shift_by_mean(k):
                nc.vector.scalar_tensor_tensor(
                    out=shift[:, quad(k)].rearrange("m (r h) -> m r h", h=2), in0=mean[:, pairs_of(k), :], scalar=-1.0,
                    in1=rstd[:, quad(k)].rearrange("m (r h) -> m r h", h=2), op0=ALU.mult, op1=ALU.mult,
                )

            def normalise(k, a, engine=None):
                if a == 0:
                    normed_of[k] = work.tile([P, 2, PACK, 2, EP], F32, name="normed")
                t = k * QUAD + a
                if engine is not None:
                    engine.tensor_scalar(
                        out=normed_of[k][:, a // 2, :, a % 2, :], in0=p_sb[:, t, :].rearrange("m (q c) -> m c q", c=PACK),
                        scalar1=rstd[:, t : t + 1], scalar2=shift[:, t : t + 1], op0=ALU.mult, op1=ALU.add,
                    )
                    return
                nc.scalar.activation(
                    out=normed_of[k][:, a // 2, :, a % 2, :], in_=p_sb[:, t, :].rearrange("m (q c) -> m c q", c=PACK),
                    func=ACT.Identity, bias=shift[:, t : t + 1], scale=rstd[:, t : t + 1],
                )

            def transpose(k):
                normed = normed_of.pop(k)
                turned = [psum_t.tile([P, 2, 2, P], F32, name="turned%d" % n) for n in range(2)]
                for c in range(PACK):
                    for pr in range(2):
                        nc.tensor.transpose(
                            out=turned[c // 2][:, c % 2, pr, :], in_=normed[:, pr, c, :, :].rearrange("m h q -> m (h q)"),
                            identity=ident[:],
                        )
                turned_of[k] = turned

            def affine(k, c, on_vector=False):
                if c == 0:
                    planes_of[k] = work.tile([P, PACK, 2 * P], BF16, name="planes")
                if on_vector:
                    nc.vector.tensor_scalar(
                        out=planes_of[k][:, c, :], in0=turned_of[k][c // 2][:, c % 2, :, :].rearrange("q r m -> q (r m)"),
                        scalar1=gain_bias[:, 0, c : c + 1], scalar2=gain_bias[:, 1, c : c + 1], op0=ALU.mult, op1=ALU.add,
                    )
                    return
                nc.scalar.activation(
                    out=planes_of[k][:, c, :], in_=turned_of[k][c // 2][:, c % 2, :, :].rearrange("q r m -> q (r m)"),
                    func=ACT.Identity, bias=gain_bias[:, 1, c : c + 1], scale=gain_bias[:, 0, c : c + 1],
                )

            def group(k, on_vector=False):
                grouped = work.tile([P, 2 * P, PACK], BF16, align_bytes=64, name="grouped")
                grouped_of[k] = grouped
                if on_vector:
                    nc.vector.tensor_copy(out=grouped[:], in_=planes_of.pop(k)[:].rearrange("q c e -> q e c"))
                    return
                nc.gpsimd.tensor_scalar(
                    out=grouped[:], in0=planes_of.pop(k)[:].rearrange("q c e -> q e c"),
                    scalar1=1.0, scalar2=0.0, op0=ALU.mult, op1=ALU.add,
                )

            def quantise(k):
                u = u_packed[k % 2]
                nc.vector.quantize_mx(
                    out=u[:, 0 : 2 * P].bitcast(FP8X4), scales=u[:, 2 * P : TWO_TILES].bitcast(U8),
                    in_=grouped_of.pop(k)[:].rearrange("q e c -> q (e c)"),
                )

            def place(k):
                for h in range(2):
                    (nc.vector.tensor_copy if h == 1 and OV(k) else nc.sync.dma_start)(out=z_packed[EP:P, k % RING, h, :], in_=u_packed[k % 2][h * EP : (h + 1) * EP, :])

            def place_of(t):
                return t // QUAD, t % 2, (t % QUAD) // 2

            def multiply(t):
                k, h, pr = place_of(t)
                for nh in range(2):
                    acc = psum_mm.tile([P, N_BANK], F32, name="acc")
                    nc.tensor.matmul_mx(
                        out=acc[:],
                        lhsT=z_packed[:, k % RING, h, pr * P : (pr + 1) * P].bitcast(FP8X4),
                        lhsT_scale=z_packed[:, k % RING, h, 2 * P + pr * P // 4 : 2 * P + (pr + 1) * P // 4].bitcast(U8),
                        rhs=w_codes[:, bank(nh)].bitcast(FP8X4), rhs_scale=w_scales[:, bank(nh)],
                        start=True, stop=True,
                    )
                    acc_of[(t, nh)] = acc

            def add_bias(t, nh):
                if nh == 0 and t % STORE == 0:
                    result_of[t // STORE] = outs.tile([P, STORE, F], F32, name="result")
                nc.vector.tensor_tensor(
                    out=result_of[t // STORE][:, t % STORE, bank(nh)], in0=acc_of.pop((t, nh))[:], in1=b1_bc[:, bank(nh)], op=ALU.add
                )

            def relu_and_store(t):
                split = SCALAR_COLS if t < LATE else LATE_COLS
                a = t % STORE
                result = result_of[t // STORE]
                paired = FIRST_PAIR <= t < WHOLE
                if paired and GP2 and a == 1:
                    nc.scalar.activation(out=result[:, a, F - split : F], in_=result[:, a, F - split : F], func=ACT.Relu)
                else:
                    nc.scalar.activation(out=result[:, a, 0:split], in_=result[:, a, 0:split], func=ACT.Relu)
                if paired and GP2:
                    if a == 1:
                        both = result[:].rearrange("m a f -> m (a f)")[:, split : 2 * F - split]
                        nc.gpsimd.tensor_scalar(
                            out=both, in0=both, scalar1=float("inf"), scalar2=0.0, op0=ALU.min, op1=ALU.max,
                        )
                else:
                    nc.gpsimd.tensor_scalar(
                        out=result[:, a, split:F], in0=result[:, a, split:F],
                        scalar1=float("inf"), scalar2=0.0, op0=ALU.min, op1=ALU.max,
                    )
                g, first = t // PER_GROUP, t % PER_GROUP - a
                if FIRST_PAIR <= t < WHOLE:
                    if a == STORE - 1:
                        nc.sync.dma_start(out=out_view[g][:, first : first + STORE, :], in_=result[:])
                else:
                    nc.sync.dma_start(out=out_view[g][:, first + a, :], in_=result[:, a, :])

            def is_quad(k):
                return 0 <= k < QUADS

            def is_tile(t):
                return 0 <= t < TILES

            def move_on_gpsimd(out, in_):
                nc.gpsimd.tensor_scalar(out=out, in0=in_, scalar1=1.0, scalar2=0.0, op0=ALU.mult, op1=ALU.add)

            def regroup_weights(piece, move):
                cols = slice(piece * W_PIECE, (piece + 1) * W_PIECE)
                move(out=w_grouped[:, cols, :], in_=w_raw[:, :, cols].rearrange("q c n -> q n c"))

            def spread_b1():
                for nh in range(2):
                    spread = psum_mm.tile([P, N_BANK], F32, name="acc")
                    nc.tensor.matmul(out=spread[:], lhsT=ones[:], rhs=b1_row[:, bank(nh)], start=True, stop=True)
                    nc.scalar.copy(out=b1_bc[:, bank(nh)], in_=spread[:])

            def at(stage, t):
                found = []
                for k in range(2, QUADS):
                    a = t - QUAD * k + (LEADS_2 if k == 2 else LEADS)[stage]
                    if 0 <= a < QUAD:
                        found.append((k, a))
                return found

            words_t = psum_mm.tile([P, 2, P], F32, name="acc")
            turn_rows(words_t)
            for pair in range(2):
                sums(pair)
            scale(0)
            keep_words(words_t)
            shift_by_mean(0)
            for a in range(QUAD):
                normalise(0, a, nc.vector if a % 2 == 1 else None)
            transpose(0)
            if NJ1 == 1:
                node_j(1, move_on_gpsimd)
            for piece in range(F // W_PIECE):
                regroup_weights(piece, move_on_gpsimd)
            if NJ1 == 2:
                node_j(1, move_on_gpsimd)
            node_j(0, nc.scalar.copy)
            for pair in range(2, 4):
                sums(pair)
            for c in range(PACK):
                affine(0, c, on_vector=c >= 2)
            scale(1)
            if NJ1 == 0:
                node_j(1, nc.scalar.copy)
            group(0, on_vector=True)
            shift_by_mean(1)
            quantise(0)
            place(0)
            if EARLY2:
                sums(4)
            node_i()
            if EARLY2:
                sums(5)
            for a in range(QUAD):
                normalise(1, a, nc.gpsimd if a < N1G else None)
            node_operands()
            if X0V:
                place_i(0, nc.vector.tensor_copy)
                place_j(0, nc.vector.tensor_copy)
            for k in range(1 if X0V else 0, RING):
                place_i(k, nc.sync.dma_start)
                place_j(k, nc.sync.dma_start)
            spread_b1()
            quantise_weights(0)
            quantise_weights(1)
            transpose(1)
            for c in range(PACK):
                affine(1, c)
            group(1)

            for t in range(-START, TILES + RELU):
                for k, a in [x for x in at("turn", t) if x[1] < 1]:
                    transpose(k)
                if is_tile(t + 2):
                    multiply(t + 2)
                if is_tile(t):
                    add_bias(t, 0)
                if t == 1:
                    quantise(1)
                    place(1)
                for k, a in [x for x in at("sums", t) if x[1] < 2]:
                    if not (EARLY2 and k == 2):
                        sums(2 * k + a)
                for k, a in [x for x in at("scale", t) if x[1] < 1]:
                    scale(k)
                for k, a in [x for x in at("quant", t) if x[1] < 1]:
                    quantise(k)
                    place(k)
                    if is_quad(k + 2) and k + 2 >= RING:
                        place_i(k + 2, nc.sync.dma_start)
                if is_tile(t):
                    add_bias(t, 1)
                for k, a in [x for x in at("shift", t) if x[1] < 1]:
                    shift_by_mean(k)
                if is_tile(t - RELU):
                    relu_and_store(t - RELU)
                for k, a in [x for x in at("norm", t) if x[1] < 2]:
                    normalise(k, 2 * a, nc.gpsimd if k == 2 and N2G > 1 else None)
                    normalise(k, 2 * a + 1, nc.gpsimd if k == 2 and N2G > 0 else None)
                for k, a in [x for x in at("affine", t) if x[1] < 2]:
                    affine(k, 2 * a)
                    affine(k, 2 * a + 1)
                for k, a in [x for x in at("group", t) if x[1] < 1]:
                    group(k, on_vector=GV(k))
